import numpy as np
import ml_dtypes


def mxq(x, axis, fmt="e4m3"):
    dtype, down = {"e4m3": (ml_dtypes.float8_e4m3fn, 7), "e5m2": (ml_dtypes.float8_e5m2, 14)}[fmt]
    v = np.moveaxis(np.asarray(x, np.float32).astype(ml_dtypes.bfloat16).astype(np.float64), axis, -1)
    blocks = v.reshape(v.shape[:-1] + (-1, 32))
    amax = np.abs(blocks).max(-1, keepdims=True)
    byte = np.maximum(np.where(amax > 0, np.frexp(amax)[1] - 1 + 127, 0) - down, 1)
    scale = np.exp2(byte - 127.0)
    codes = (blocks / scale).astype(np.float32).astype(dtype).astype(np.float64)
    return np.moveaxis((codes * scale).reshape(v.shape), -1, axis)


WIDE = False


def mx_kscale(k):
    if not WIDE:
        return np.ones(k)
    levels = np.array([10, -10, 5, -5, 0])
    a = np.random.permutation(np.resize(levels, k // 512 * 4)).reshape(k // 512, 4)
    idx = np.arange(k)
    return np.exp2(a[idx // 512, idx % 128 // 32])


BF16 = ml_dtypes.bfloat16


def bf(x):
    return np.asarray(x, np.float32).astype(BF16)


def f64(x):
    return np.asarray(x).astype(np.float64)


B, S, D, K, O, DEG, BLK = 4, 128, 1536, 1536, 2048, 6, 512
HALF = DEG // 2
STEP = K // DEG
KH = HALF * STEP


def make_masks(lo, hi):
    rows = np.arange(K)
    deg_r = (rows * DEG) // K + 1
    degmask = (np.arange(1, DEG + 1)[:, None] <= deg_r[None, :]) * 1.0
    tri_l = np.tril(np.ones((K, D)))
    tri_u = np.triu(np.ones((K, D)))
    return np.stack([degmask[i][:, None] * (tri_l if i % 2 == 0 else tri_u) for i in range(lo, hi)])


def factor(zq, Wi, i):
    y = np.zeros((zq.shape[0], K))
    for j in range(K // BLK):
        a, b = max(j * BLK, i * STEP), (j + 1) * BLK
        c0, c1 = (0, min(b, D)) if i % 2 == 0 else (j * BLK, D)
        if a >= b or c0 >= c1:
            continue
        y[:, a:b] = zq[:, c0:c1] @ mxq(Wi[a - KH:b - KH, c0:c1], 1, "e4m3").T
    return y


def setup_inputs():
    s, t = mx_kscale(D), mx_kscale(K)
    return {"z": bf(np.random.standard_normal((B, S, D)) * s),
            "chain_lo": bf(np.random.standard_normal((B * S, K)) * t),
            "U_hi": bf(np.random.standard_normal((DEG - HALF, K - KH, D)) / np.sqrt(D) / s),
            "masks_hi": bf(make_masks(HALF, DEG)[:, KH:, :]),
            "C_w": bf(np.random.standard_normal((O, K)) / np.sqrt(K) / t),
            "C_b": bf(np.random.standard_normal(O) * 0.5)}


def reference(z, chain_lo, U_hi, masks_hi, C_w, C_b):
    lead = z.shape[:-1]
    zq = mxq(f64(z).reshape(-1, D), 1, "e4m3")
    W = f64(masks_hi) * f64(U_hi)
    out = f64(chain_lo)
    for i in range(HALF, DEG):
        out = factor(zq, W[i - HALF], i) * out + out
    x = (mxq(out, 1, "e4m3") @ mxq(f64(C_w), 1, "e4m3").T) + f64(C_b)
    return x.reshape(*lead, O)

@@ -1,0 +1,319 @@
+from contextlib import ExitStack
+
+import concourse.mybir as mybir
+from concourse.masks import make_identity
+
+F32 = mybir.dt.float32
+BF16 = mybir.dt.bfloat16
+U32 = mybir.dt.uint32
+U8 = mybir.dt.uint8
+I32 = mybir.dt.int32
+FP8X4 = mybir.dt.float8_e4m3fn_x4
+ADD = mybir.AluOpType.add
+MULT = mybir.AluOpType.mult
+
+P = 128
+FEATURES = 1536
+RANKS = 1536
+OUTS = 2048
+FIRST_RANK = 768
+
+FLOPS = 2 * 512 * (1441792 + OUTS * RANKS)
+
+FACTOR_BLOCKS = ((5, 5, 1280, 1536), (3, 5, 1280, 1536), (3, 4, 1024, 1536), (3, 3, 768, 1536),
+                 (4, 4, 0, 1280), (4, 5, 0, 1536))
+FACTOR_PASSES = {(5, 5): (2,), (3, 5): (2,), (3, 4): (2,), (3, 3): (1, 2), (4, 4): (0, 1, 2), (4, 5): (0, 1, 2)}
+
+MANUAL = True
+
+
+def tile_cp_sparse_degree_lu_pb_kernel(tc, z, chain_lo, U_hi, masks_hi, C_w, C_b, out):
+    nc = tc.nc
+    zf = z.flatten_outer_dims()
+    of = out.flatten_outer_dims()
+    with ExitStack() as ctx:
+        if MANUAL:
+            ctx.enter_context(tc.manual_schedule())
+        const = ctx.enter_context(tc.tile_pool(name="const", bufs=1))
+        raw = ctx.enter_context(tc.tile_pool(name="raw", bufs=1))
+        keep = ctx.enter_context(tc.tile_pool(name="keep", bufs=1))
+        grp = ctx.enter_context(tc.tile_pool(name="grp", bufs=6))
+        tmp = ctx.enter_context(tc.tile_pool(name="tmp", bufs=2))
+        stage = ctx.enter_context(tc.tile_pool(name="stage", bufs=6))
+        tp = ctx.enter_context(tc.psum_pool(name="tp", bufs=4))
+        acc = ctx.enter_context(tc.psum_pool(name="acc", bufs=4))
+
+        ident = const.tile([P, P], F32, name="ident")
+        make_identity(nc, ident[:])
+        zero_words = const.tile([P, P], F32, name="zero_words")
+        nc.vector.memset(zero_words[:], 0.0)
+        ones = const.tile([P, P], BF16, name="ones")
+        nc.vector.memset(ones[:], 1.0)
+        bias_row = const.tile([P, OUTS], BF16, name="bias_row")
+        nc.vector.memset(bias_row[:].bitcast(I32), 0)
+        nc.scalar.dma_start(out=bias_row[0:1, :], in_=C_b.unsqueeze(0))
+        bias = const.tile([P, OUTS], F32, name="bias")
+
+        def load_rows(name, rows):
+            t = raw.tile([P, 2, rows.shape[1]], BF16, name=name)
+            nc.sync.dma_start(out=t[:], in_=rows.rearrange("(a p) c -> p a c", p=P))
+            return t
+
+        u_raw = {}
+        m_raw = {}
+
+        def load_factor(i, blk, c0, c1):
+            r0 = 256 * blk - FIRST_RANK
+            m = raw.tile([P, 2, 256], BF16, name="m%d%d" % (i, blk))
+            nc.sync.dma_start(
+                out=m[:],
+                in_=masks_hi[i - 3, r0:r0 + 256, 256 * blk:256 * blk + 256].rearrange("(m e) c -> m e c", e=2))
+            u = raw.tile([P, 2, c1 - c0], BF16, name="u%d%d" % (i, blk))
+            nc.sync.dma_start(out=u[:], in_=U_hi[i - 3, r0:r0 + 256, c0:c1].rearrange("(m e) c -> m e c", e=2))
+            u_raw[(i, blk)] = u
+            m_raw[(i, blk)] = m
+
+        z_raw = {}
+        ch_raw = {}
+        z_raw[0] = load_rows("z0", zf[0:256, :])
+        ch_raw[0] = load_rows("ch0", chain_lo[0:256, :])
+        for (i, blk, c0, c1) in FACTOR_BLOCKS:
+            load_factor(i, blk, c0, c1)
+        z_raw[1] = load_rows("z1", zf[256:512, :])
+        ch_raw[1] = load_rows("ch1", chain_lo[256:512, :])
+        cw_raw = [load_rows("cw%d" % q, C_w[256 * q:256 * q + 256, :]) for q in range(8)]
+
+        for j in range(4):
+            spread = acc.tile([P, 512], F32, name="spread%d" % j, tag="acc")
+            nc.tensor.matmul(out=spread[:], lhsT=ones[:], rhs=bias_row[:, 512 * j:512 * j + 512], start=True, stop=True)
+            nc.scalar.copy(out=bias[:, 512 * j:512 * j + 512], in_=spread[:])
+
+        def transposes(name, sources):
+            bank = tp.tile([P, 2, 2, P], F32, name="tp_" + name, tag="tp")
+            for a in range(2):
+                for u in range(2):
+                    nc.tensor.transpose(bank[:, a, u, :], sources[a][u], ident[:])
+            return bank
+
+        def regroup(bank, grouped):
+            nc.scalar.copy(out=grouped[:].bitcast(F32).rearrange("p (a m u) -> p a m u", a=2, u=2),
+                           in_=bank[:].rearrange("p a u m -> p a m u"))
+
+        def quantise(grouped, codes, scales):
+            nc.vector.quantize_mx(out=codes.bitcast(FP8X4), scales=scales, in_=grouped[:])
+
+        def words(tile_ap, a, first_word):
+            return tile_ap[:].bitcast(F32)[:, a, first_word:first_word + P]
+
+        def row_sources(tile_ap, g):
+            return [[words(tile_ap, a, 256 * g + 128 * u) for u in range(2)] for a in range(2)]
+
+        zc = {}
+        zs = {}
+        wc = {}
+        ws = {}
+        oc = {}
+        osc = {}
+        cc = {}
+        cs = {}
+        ct = {}
+
+        def z_unit(pair, g):
+            bank = transposes("z%d%d" % (pair, g), row_sources(z_raw[pair], g))
+            grouped = grp.tile([P, 1024], BF16, name="gz%d%d" % (pair, g), tag="grp", align_bytes=64)
+            regroup(bank, grouped)
+            zc[(g, pair)] = keep.tile([P, 256], U32, name="zc%d%d" % (g, pair), align_bytes=64)
+            zs[(g, pair)] = keep.tile([P, 256], U8, name="zs%d%d" % (g, pair), align_bytes=64)
+            return lambda: quantise(grouped, zc[(g, pair)][:], zs[(g, pair)][:])
+
+        def chain_unit(pair, g):
+            bank = transposes("c%d%d" % (pair, g), row_sources(ch_raw[pair], g))
+            ct[(g, pair)] = keep.tile([P, 1024], BF16, name="ct%d%d" % (g, pair), align_bytes=64)
+            regroup(bank, ct[(g, pair)])
+            oc[(g, pair)] = keep.tile([P, 256], U32, name="oc%d%d" % (g, pair), align_bytes=64)
+            osc[(g, pair)] = keep.tile([P, 256], U8, name="os%d%d" % (g, pair), align_bytes=64)
+
+        def chain_quantise(pair, g):
+            quantise(ct[(g, pair)], oc[(g, pair)][:], osc[(g, pair)][:])
+
+        def apply_mask(i, blk, c0):
+            d0 = 256 * blk - c0
+            u = u_raw[(i, blk)]
+            nc.vector.tensor_tensor(out=u[:, :, d0:d0 + 256], in0=u[:, :, d0:d0 + 256], in1=m_raw[(i, blk)][:], op=MULT)
+
+        def factor_unit(i, blk, c0, c1, g):
+            sources = []
+            for e in range(2):
+                row = []
+                for u in range(2):
+                    c = 512 * g + 256 * u
+                    if c0 <= c < c1:
+                        row.append(words(u_raw[(i, blk)], e, (c - c0) // 2))
+                    else:
+                        row.append(zero_words[:])
+                sources.append(row)
+            bank = transposes("w%d%d%d" % (i, blk, g), sources)
+            grouped = grp.tile([P, 1024], BF16, name="gw%d%d%d" % (i, blk, g), tag="grp", align_bytes=64)
+            regroup(bank, grouped)
+            wc[(i, blk, g)] = keep.tile([P, 256], U32, name="wc%d%d%d" % (i, blk, g), align_bytes=64)
+            ws[(i, blk, g)] = keep.tile([P, 256], U8, name="ws%d%d%d" % (i, blk, g), align_bytes=64)
+            return lambda: quantise(grouped, wc[(i, blk, g)][:], ws[(i, blk, g)][:])
+
+        def cw_unit(q, g):
+            j, h = divmod(q, 2)
+            bank = transposes("cw%d%d" % (q, g), row_sources(cw_raw[q], g))
+            grouped = grp.tile([P, 1024], BF16, name="gc%d%d" % (q, g), tag="grp", align_bytes=64)
+            regroup(bank, grouped)
+            if h == 0:
+                cc[(j, g)] = keep.tile([P, 512], U32, name="cc%d%d" % (j, g), align_bytes=64)
+                cs[(j, g)] = keep.tile([P, 512], U8, name="cs%d%d" % (j, g), align_bytes=64)
+            return lambda: quantise(grouped, cc[(j, g)][:, 256 * h:256 * h + 256], cs[(j, g)][:, 256 * h:256 * h + 256])
+
+        def factor_bank(i, blk, pair):
+            y = acc.tile([P, 2, 256], F32, name="y%d%d%d" % (i, blk, pair), tag="acc")
+            passes = FACTOR_PASSES[(i, blk)]
+            for e in range(2):
+                for g in passes:
+                    nc.tensor.matmul_mx(
+                        out=y[:, e, :],
+                        lhsT=wc[(i, blk, g)][:, P * e:P * e + P].bitcast(FP8X4),
+                        lhsT_scale=ws[(i, blk, g)][:, P * e:P * e + P],
+                        rhs=zc[(g, pair)][:].bitcast(FP8X4),
+                        rhs_scale=zs[(g, pair)][:],
+                        start=(g == passes[0]),
+                        stop=(g == passes[-1]),
+                    )
+            return y
+
+        def multiply_in(dst, y, src):
+            nc.vector.scalar_tensor_tensor(out=dst, in0=y[:].rearrange("p e n -> p n e"), scalar=1.0, in1=src,
+                                           op0=ADD, op1=MULT)
+
+        def half(pair, g, u):
+            return ct[(g, pair)][:].rearrange("p (n t) -> p n t", t=4)[:, :, 2 * u:2 * u + 2]
+
+        def project(j, nt):
+            pair, k = divmod(nt, 2)
+            x = acc.tile([P, 512], F32, name="x%d%d" % (j, nt), tag="acc")
+            for g in range(3):
+                nc.tensor.matmul_mx(
+                    out=x[:],
+                    lhsT=oc[(g, pair)][:, P * k:P * k + P].bitcast(FP8X4),
+                    lhsT_scale=osc[(g, pair)][:, P * k:P * k + P],
+                    rhs=cc[(j, g)][:].bitcast(FP8X4),
+                    rhs_scale=cs[(j, g)][:],
+                    start=(g == 0),
+                    stop=(g == 2),
+                )
+            return x
+
+        def finish(j, nt, x):
+            res = stage.tile([P, 512], F32, name="res%d%d" % (j, nt), tag="res")
+            nc.vector.tensor_tensor(out=res[:], in0=x[:], in1=bias[:, 512 * j:512 * j + 512], op=ADD)
+            nc.sync.dma_start(out=of[P * nt:P * nt + P, 512 * j:512 * j + 512], in_=res[:])
+
+
+        FB = {(i, blk): (c0, c1) for (i, blk, c0, c1) in FACTOR_BLOCKS}
+
+        def funit(i, blk, g):
+            return factor_unit(i, blk, FB[(i, blk)][0], FB[(i, blk)][1], g)
+
+        def mask(i, blk):
+            apply_mask(i, blk, FB[(i, blk)][0])
+
+        part = {}
+
+        def new_part(name, pair):
+            part[(name, pair)] = tmp.tile([P, 256, 2], F32, name="%s%d" % (name, pair), tag=name)
+            return part[(name, pair)]
+
+        for g in range(3):
+            z_unit(0, g)()
+        for g in (2, 1, 0):
+            chain_unit(0, g)
+        mask(5, 5)
+        mask(3, 5)
+        q55 = funit(5, 5, 2)
+        q35 = funit(3, 5, 2)
+        chain_quantise(0, 0)
+        q55()
+        mask(3, 4)
+        q35()
+        y55 = factor_bank(5, 5, 0)
+        q34 = funit(3, 4, 2)
+        multiply_in(new_part("hi", 0)[:], y55, half(0, 2, 1))
+        mask(3, 3)
+        q34()
+        y35 = factor_bank(3, 5, 0)
+        q331 = funit(3, 3, 1)
+        q332 = funit(3, 3, 2)
+        multiply_in(part[("hi", 0)][:], y35, part[("hi", 0)][:])
+        q331()
+        q332()
+        y34 = factor_bank(3, 4, 0)
+        mask(4, 4)
+        q440 = funit(4, 4, 0)
+        multiply_in(new_part("lo", 0)[:], y34, half(0, 2, 0))
+        y33 = factor_bank(3, 3, 0)
+        q441 = funit(4, 4, 1)
+        q442 = funit(4, 4, 2)
+        q440()
+        multiply_in(half(0, 1, 1), y33, half(0, 1, 1))
+        chain_quantise(0, 1)
+        q441()
+        q442()
+        mask(4, 5)
+        q450 = funit(4, 5, 0)
+        q451 = funit(4, 5, 1)
+        q450()
+        q451()
+        y44 = factor_bank(4, 4, 0)
+        q452 = funit(4, 5, 2)
+        qz10 = z_unit(1, 0)
+        qz11 = z_unit(1, 1)
+        q452()
+        multiply_in(half(0, 2, 0), y44, part[("lo", 0)][:])
+        qz10()
+        qz11()
+        y45 = factor_bank(4, 5, 0)
+        qz12 = z_unit(1, 2)
+        for g in (2, 1, 0):
+            chain_unit(1, g)
+        qz12()
+        multiply_in(half(0, 2, 1), y45, part[("hi", 0)][:])
+        chain_quantise(0, 2)
+        chain_quantise(1, 0)
+        y55 = factor_bank(5, 5, 1)
+        y35 = factor_bank(3, 5, 1)
+        y45 = factor_bank(4, 5, 1)
+        y34 = factor_bank(3, 4, 1)
+        qc = [cw_unit(0, g) for g in range(3)]
+        multiply_in(new_part("hi", 1)[:], y55, half(1, 2, 1))
+        multiply_in(part[("hi", 1)][:], y35, part[("hi", 1)][:])
+        qc[0]()
+        multiply_in(half(1, 2, 1), y45, part[("hi", 1)][:])
+        qc[1]()
+        multiply_in(new_part("lo", 1)[:], y34, half(1, 2, 0))
+        qc[2]()
+        y44 = factor_bank(4, 4, 1)
+        y33 = factor_bank(3, 3, 1)
+        qc = [cw_unit(1, g) for g in range(3)]
+        multiply_in(half(1, 2, 0), y44, part[("lo", 1)][:])
+        chain_quantise(1, 2)
+        qc[0]()
+        multiply_in(half(1, 1, 1), y33, half(1, 1, 1))
+        chain_quantise(1, 1)
+        qc[1]()
+        qc[2]()
+        for j in range(1, 5):
+            qc = []
+            if j < 4:
+                qc = [cw_unit(2 * j + h, g) for h in range(2) for g in range(3)]
+            for q in qc[:4]:
+                q()
+            for nt in range(4):
+                x = project(j - 1, nt)
+                finish(j - 1, nt, x)
+                if nt == 0:
+                    for q in qc[4:]:
+                        q()

@@ -19,6 +19,7 @@ OUTS = 2048
 FIRST_RANK = 768
 
 FLOPS = 2 * 512 * (1441792 + OUTS * RANKS)
+BYTES = 2 * (2 * 512 * 1536 + 36 * 128 * 256 + 12 * 128 * 256 + OUTS * RANKS + OUTS) + 4 * 512 * OUTS
 
 FACTOR_BLOCKS = ((5, 5, 1280, 1536), (3, 5, 1280, 1536), (3, 4, 1024, 1536), (3, 3, 768, 1536),
                  (4, 4, 0, 1280), (4, 5, 0, 1536))
@@ -75,12 +76,23 @@ def tile_cp_sparse_degree_lu_pb_kernel(tc, z, chain_lo, U_hi, masks_hi, C_w, C_b
 
         z_raw = {}
         ch_raw = {}
-        z_raw[0] = load_rows("z0", zf[0:256, :])
-        ch_raw[0] = load_rows("ch0", chain_lo[0:256, :])
-        for (i, blk, c0, c1) in FACTOR_BLOCKS:
+
+        def load_split(store, name, src, part_name, pair):
+            c0, c1 = (512, 1536) if part_name == "hi" else (0, 512)
+            store[(part_name, pair)] = load_rows("%s%s%d" % (name, part_name, pair), src[256 * pair:256 * pair + 256, c0:c1])
+
+        for pair in range(2):
+            load_split(z_raw, "z", zf, "hi", pair)
+        for pair in range(2):
+            load_split(ch_raw, "ch", chain_lo, "hi", pair)
+        for (i, blk, c0, c1) in FACTOR_BLOCKS[:4]:
             load_factor(i, blk, c0, c1)
-        z_raw[1] = load_rows("z1", zf[256:512, :])
-        ch_raw[1] = load_rows("ch1", chain_lo[256:512, :])
+        for pair in range(2):
+            load_split(z_raw, "z", zf, "lo", pair)
+        for (i, blk, c0, c1) in FACTOR_BLOCKS[4:]:
+            load_factor(i, blk, c0, c1)
+        for pair in range(2):
+            load_split(ch_raw, "ch", chain_lo, "lo", pair)
         cw_raw = [load_rows("cw%d" % q, C_w[256 * q:256 * q + 256, :]) for q in range(8)]
 
         for j in range(4):
@@ -108,6 +120,11 @@ def tile_cp_sparse_degree_lu_pb_kernel(tc, z, chain_lo, U_hi, masks_hi, C_w, C_b
         def row_sources(tile_ap, g):
             return [[words(tile_ap, a, 256 * g + 128 * u) for u in range(2)] for a in range(2)]
 
+        def split_sources(tiles, pair, g):
+            if g == 0:
+                return row_sources(tiles[("lo", pair)], 0)
+            return row_sources(tiles[("hi", pair)], g - 1)
+
         zc = {}
         zs = {}
         wc = {}
@@ -119,7 +136,7 @@ def tile_cp_sparse_degree_lu_pb_kernel(tc, z, chain_lo, U_hi, masks_hi, C_w, C_b
         ct = {}
 
         def z_unit(pair, g):
-            bank = transposes("z%d%d" % (pair, g), row_sources(z_raw[pair], g))
+            bank = transposes("z%d%d" % (pair, g), split_sources(z_raw, pair, g))
             grouped = grp.tile([P, 1024], BF16, name="gz%d%d" % (pair, g), tag="grp", align_bytes=64)
             regroup(bank, grouped)
             zc[(g, pair)] = keep.tile([P, 256], U32, name="zc%d%d" % (g, pair), align_bytes=64)
@@ -127,7 +144,7 @@ def tile_cp_sparse_degree_lu_pb_kernel(tc, z, chain_lo, U_hi, masks_hi, C_w, C_b
             return lambda: quantise(grouped, zc[(g, pair)][:], zs[(g, pair)][:])
 
         def chain_unit(pair, g):
-            bank = transposes("c%d%d" % (pair, g), row_sources(ch_raw[pair], g))
+            bank = transposes("c%d%d" % (pair, g), split_sources(ch_raw, pair, g))
             ct[(g, pair)] = keep.tile([P, 1024], BF16, name="ct%d%d" % (g, pair), align_bytes=64)
             regroup(bank, ct[(g, pair)])
             oc[(g, pair)] = keep.tile([P, 256], U32, name="oc%d%d" % (g, pair), align_bytes=64)
@@ -139,7 +156,7 @@ def tile_cp_sparse_degree_lu_pb_kernel(tc, z, chain_lo, U_hi, masks_hi, C_w, C_b
         def apply_mask(i, blk, c0):
             d0 = 256 * blk - c0
             u = u_raw[(i, blk)]
-            nc.vector.tensor_tensor(out=u[:, :, d0:d0 + 256], in0=u[:, :, d0:d0 + 256], in1=m_raw[(i, blk)][:], op=MULT)
+            nc.gpsimd.tensor_tensor(out=u[:, :, d0:d0 + 256], in0=u[:, :, d0:d0 + 256], in1=m_raw[(i, blk)][:], op=MULT)
 
         def factor_unit(i, blk, c0, c1, g):
             sources = []
@@ -214,6 +231,7 @@ def tile_cp_sparse_degree_lu_pb_kernel(tc, z, chain_lo, U_hi, masks_hi, C_w, C_b
 
 
         FB = {(i, blk): (c0, c1) for (i, blk, c0, c1) in FACTOR_BLOCKS}
+        PAIRS = (0, 1)
 
         def funit(i, blk, g):
             return factor_unit(i, blk, FB[(i, blk)][0], FB[(i, blk)][1], g)
@@ -221,99 +239,90 @@ def tile_cp_sparse_degree_lu_pb_kernel(tc, z, chain_lo, U_hi, masks_hi, C_w, C_b
         def mask(i, blk):
             apply_mask(i, blk, FB[(i, blk)][0])
 
-        part = {}
+        def banks(i, blk):
+            return [factor_bank(i, blk, pair) for pair in PAIRS]
 
-        def new_part(name, pair):
-            part[(name, pair)] = tmp.tile([P, 256, 2], F32, name="%s%d" % (name, pair), tag=name)
-            return part[(name, pair)]
+        hi = [tmp.tile([P, 256, 2], F32, name="hi%d" % pair) for pair in PAIRS]
+        lo = [tmp.tile([P, 256, 2], F32, name="lo%d" % pair) for pair in PAIRS]
 
-        for g in range(3):
-            z_unit(0, g)()
-        for g in (2, 1, 0):
-            chain_unit(0, g)
+        for g in (2, 1):
+            for pair in PAIRS:
+                z_unit(pair, g)()
+        for g in (2, 1):
+            for pair in PAIRS:
+                chain_unit(pair, g)
         mask(5, 5)
         mask(3, 5)
         q55 = funit(5, 5, 2)
         q35 = funit(3, 5, 2)
-        chain_quantise(0, 0)
         q55()
         mask(3, 4)
         q35()
-        y55 = factor_bank(5, 5, 0)
+        y = banks(5, 5)
         q34 = funit(3, 4, 2)
-        multiply_in(new_part("hi", 0)[:], y55, half(0, 2, 1))
+        for pair in PAIRS:
+            multiply_in(hi[pair][:], y[pair], half(pair, 2, 1))
         mask(3, 3)
         q34()
-        y35 = factor_bank(3, 5, 0)
+        y = banks(3, 5)
         q331 = funit(3, 3, 1)
         q332 = funit(3, 3, 2)
-        multiply_in(part[("hi", 0)][:], y35, part[("hi", 0)][:])
+        for pair in PAIRS:
+            multiply_in(hi[pair][:], y[pair], hi[pair][:])
         q331()
         q332()
-        y34 = factor_bank(3, 4, 0)
+        y = banks(3, 4)
+        qz = [z_unit(pair, 0) for pair in PAIRS]
+        for pair in PAIRS:
+            multiply_in(lo[pair][:], y[pair], half(pair, 2, 0))
         mask(4, 4)
-        q440 = funit(4, 4, 0)
-        multiply_in(new_part("lo", 0)[:], y34, half(0, 2, 0))
-        y33 = factor_bank(3, 3, 0)
-        q441 = funit(4, 4, 1)
-        q442 = funit(4, 4, 2)
-        q440()
-        multiply_in(half(0, 1, 1), y33, half(0, 1, 1))
-        chain_quantise(0, 1)
-        q441()
-        q442()
+        y = [factor_bank(3, 3, 0)]
+        q44 = [funit(4, 4, g) for g in range(3)]
+        y.append(factor_bank(3, 3, 1))
+        for q in qz:
+            q()
+        multiply_in(half(0, 1, 1), y[0], half(0, 1, 1))
+        for q in q44:
+            q()
+        multiply_in(half(1, 1, 1), y[1], half(1, 1, 1))
         mask(4, 5)
-        q450 = funit(4, 5, 0)
-        q451 = funit(4, 5, 1)
-        q450()
-        q451()
-        y44 = factor_bank(4, 4, 0)
-        q452 = funit(4, 5, 2)
-        qz10 = z_unit(1, 0)
-        qz11 = z_unit(1, 1)
-        q452()
-        multiply_in(half(0, 2, 0), y44, part[("lo", 0)][:])
-        qz10()
-        qz11()
-        y45 = factor_bank(4, 5, 0)
-        qz12 = z_unit(1, 2)
-        for g in (2, 1, 0):
-            chain_unit(1, g)
-        qz12()
-        multiply_in(half(0, 2, 1), y45, part[("hi", 0)][:])
+        q45 = [funit(4, 5, g) for g in range(3)]
+        y = [factor_bank(4, 4, 0)]
+        for q in q45:
+            q()
+        for pair in PAIRS:
+            chain_unit(pair, 0)
+        y.append(factor_bank(4, 4, 1))
+        for pair in PAIRS:
+            multiply_in(half(pair, 2, 0), y[pair], lo[pair][:])
+        qc = [cw_unit(0, g) for g in (0, 1)]
+        y = [factor_bank(4, 5, 0)]
+        for pair in PAIRS:
+            chain_quantise(pair, 1)
+            chain_quantise(pair, 0)
+        for q in qc:
+            q()
+        qc = [cw_unit(0, 2), cw_unit(1, 0)]
+        y.append(factor_bank(4, 5, 1))
+        multiply_in(half(0, 2, 1), y[0], hi[0][:])
         chain_quantise(0, 2)
-        chain_quantise(1, 0)
-        y55 = factor_bank(5, 5, 1)
-        y35 = factor_bank(3, 5, 1)
-        y45 = factor_bank(4, 5, 1)
-        y34 = factor_bank(3, 4, 1)
-        qc = [cw_unit(0, g) for g in range(3)]
-        multiply_in(new_part("hi", 1)[:], y55, half(1, 2, 1))
-        multiply_in(part[("hi", 1)][:], y35, part[("hi", 1)][:])
-        qc[0]()
-        multiply_in(half(1, 2, 1), y45, part[("hi", 1)][:])
-        qc[1]()
-        multiply_in(new_part("lo", 1)[:], y34, half(1, 2, 0))
-        qc[2]()
-        y44 = factor_bank(4, 4, 1)
-        y33 = factor_bank(3, 3, 1)
-        qc = [cw_unit(1, g) for g in range(3)]
-        multiply_in(half(1, 2, 0), y44, part[("lo", 1)][:])
+        for q in qc:
+            q()
+        multiply_in(half(1, 2, 1), y[1], hi[1][:])
         chain_quantise(1, 2)
-        qc[0]()
-        multiply_in(half(1, 1, 1), y33, half(1, 1, 1))
-        chain_quantise(1, 1)
-        qc[1]()
-        qc[2]()
-        for j in range(1, 5):
+        qc = [cw_unit(1, g) for g in (1, 2)]
+        for q in qc:
+            q()
+        for step in range(2, 10):
             qc = []
-            if j < 4:
-                qc = [cw_unit(2 * j + h, g) for h in range(2) for g in range(3)]
-            for q in qc[:4]:
+            if step < 8:
+                qc = [cw_unit(step, g) for g in range(3)]
+            j, h = divmod(step - 2, 2)
+            for q in qc[:2]:
                 q()
-            for nt in range(4):
-                x = project(j - 1, nt)
-                finish(j - 1, nt, x)
-                if nt == 0:
-                    for q in qc[4:]:
+            for nt in (2 * h, 2 * h + 1):
+                x = project(j, nt)
+                finish(j, nt, x)
+                if nt == 2 * h:
+                    for q in qc[2:]:
                         q()

@@ -13,7 +13,6 @@ ADD = mybir.AluOpType.add
 MULT = mybir.AluOpType.mult
 
 P = 128
-FEATURES = 1536
 RANKS = 1536
 OUTS = 2048
 FIRST_RANK = 768
@@ -21,11 +20,45 @@ FIRST_RANK = 768
 FLOPS = 2 * 512 * (1441792 + OUTS * RANKS)
 BYTES = 2 * (2 * 512 * 1536 + 36 * 128 * 256 + 12 * 128 * 256 + OUTS * RANKS + OUTS) + 4 * 512 * OUTS
 
-FACTOR_BLOCKS = ((5, 5, 1280, 1536), (3, 5, 1280, 1536), (3, 4, 1024, 1536), (3, 3, 768, 1536),
-                 (4, 4, 0, 1280), (4, 5, 0, 1536))
-FACTOR_PASSES = {(5, 5): (2,), (3, 5): (2,), (3, 4): (2,), (3, 3): (1, 2), (4, 4): (0, 1, 2), (4, 5): (0, 1, 2)}
-
+ALIVE = {(5, 5): (1280, 1536), (3, 5): (1280, 1536), (3, 4): (1024, 1536), (3, 3): (768, 1536), (4, 4): (0, 1280),
+         (4, 5): (0, 1536)}
+PASSES = {(5, 5): (2,), (3, 5): (2,), (3, 4): (2,), (3, 3): (1, 2), (4, 4): (0, 1, 2), (4, 5): (0, 1, 2)}
 MANUAL = True
+TP_BUFS = 4
+ACC_BUFS = 4
+LOAD_ORDER = (
+    "zhi0", "zhi1", "M55", "U55", "M35", "U35", "M34", "U34", "chi0", "chi1", "M33", "U33", "zlo0", "zlo1", "M44",
+    "U44", "M45", "U45", "clo0", "clo1", "cw0", "cw1", "cw2", "cw3", "cw4", "cw5", "cw6", "cw7",
+)
+ORDER = (
+    ("T", "z20"), ("T", "z10"), ("C", "z20"), ("T", "z21"), ("C", "z10"), ("Q", "z20"), ("T", "z11"), ("C", "z21"),
+    ("Q", "z10"), ("B", "0"), ("C", "z11"), ("Q", "z21"), ("B", "1"), ("Q", "z11"), ("BC", "0"), ("B", "2"), ("BC",
+    "1"), ("T", "w552"), ("BC", "2"), ("B", "3"), ("C", "w552"), ("T", "w352"), ("BC", "3"), ("T", "w342"), ("Q",
+    "w552"), ("T", "c20"), ("C", "w352"), ("Y", "550"), ("T", "c10"), ("C", "w342"), ("Q", "w352"), ("T", "c21"),
+    ("C", "c20"), ("T", "c11"), ("Y", "551"), ("C", "c10"), ("M", "hi550"), ("Y", "350"), ("C", "c21"), ("Y",
+    "351"), ("Q", "w342"), ("T", "w331"), ("C", "c11"), ("M", "hi551"), ("Y", "340"), ("C", "w331"), ("T", "w332"),
+    ("M", "hi350"), ("T", "z00"), ("Q", "w331"), ("C", "w332"), ("T", "z01"), ("M", "hi351"), ("T", "w440"), ("C",
+    "z00"), ("T", "w441"), ("Q", "w332"), ("Y", "341"), ("C", "z01"), ("Q", "z00"), ("Y", "330"), ("M", "lo340"),
+    ("C", "w440"), ("T", "w442"), ("Q", "z01"), ("C", "w441"), ("M", "lo341"), ("T", "w450"), ("C", "w442"), ("T",
+    "w451"), ("Q", "w440"), ("Y", "331"), ("C", "w450"), ("Q", "w441"), ("Q", "w442"), ("C", "w451"), ("Y", "440"),
+    ("M", "o330"), ("T", "w452"), ("Q", "w450"), ("M", "o331"), ("T", "c00"), ("C", "w452"), ("T", "c01"), ("T",
+    "k00"), ("O", "10"), ("C", "c00"), ("Y", "441"), ("C", "c01"), ("O", "00"), ("Q", "w451"), ("C", "k00"), ("T",
+    "k01"), ("Q", "w452"), ("T", "k02"), ("O", "11"), ("C", "k01"), ("O", "01"), ("T", "k10"), ("Q", "k00"), ("T",
+    "k11"), ("C", "k02"), ("Q", "k01"), ("T", "k12"), ("M", "o440"), ("Y", "450"), ("C", "k10"), ("C", "k11"),
+    ("M", "o441"), ("T", "k20"), ("C", "k12"), ("T", "k21"), ("Q", "k02"), ("C", "k20"), ("T", "k22"), ("Q",
+    "k10"), ("Y", "451"), ("C", "k21"), ("M", "o450"), ("C", "k22"), ("T", "k30"), ("O", "20"), ("T", "k31"), ("Q",
+    "k11"), ("C", "k30"), ("Q", "k12"), ("T", "k32"), ("Q", "k20"), ("T", "k40"), ("C", "k31"), ("Q", "k21"), ("T",
+    "k41"), ("Q", "k22"), ("X", "00"), ("C", "k32"), ("C", "k40"), ("X", "01"), ("C", "k41"), ("E", "00"), ("T",
+    "k42"), ("Q", "k30"), ("Q", "k31"), ("T", "k50"), ("M", "o451"), ("C", "k42"), ("T", "k51"), ("T", "k52"),
+    ("C", "k50"), ("T", "k60"), ("Q", "k32"), ("O", "21"), ("X", "02"), ("C", "k51"), ("Q", "k40"), ("C", "k52"),
+    ("Q", "k41"), ("X", "03"), ("Q", "k42"), ("C", "k60"), ("Q", "k50"), ("E", "01"), ("X", "10"), ("E", "02"),
+    ("X", "11"), ("E", "03"), ("E", "10"), ("X", "12"), ("Q", "k51"), ("E", "11"), ("T", "k61"), ("T", "k62"),
+    ("Q", "k52"), ("C", "k61"), ("T", "k70"), ("E", "12"), ("T", "k71"), ("C", "k62"), ("T", "k72"), ("Q", "k60"),
+    ("X", "13"), ("Q", "k61"), ("C", "k70"), ("Q", "k62"), ("C", "k71"), ("X", "20"), ("C", "k72"), ("E", "13"),
+    ("X", "21"), ("Q", "k70"), ("E", "20"), ("X", "22"), ("E", "21"), ("X", "23"), ("Q", "k71"), ("Q", "k72"),
+    ("E", "22"), ("X", "30"), ("E", "23"), ("X", "31"), ("E", "30"), ("X", "32"), ("E", "31"), ("X", "33"), ("E",
+    "32"), ("E", "33"),
+)
 
 
 def tile_cp_sparse_degree_lu_pb_kernel(tc, z, chain_lo, U_hi, masks_hi, C_w, C_b, out):
@@ -39,10 +72,9 @@ def tile_cp_sparse_degree_lu_pb_kernel(tc, z, chain_lo, U_hi, masks_hi, C_w, C_b
         raw = ctx.enter_context(tc.tile_pool(name="raw", bufs=1))
         keep = ctx.enter_context(tc.tile_pool(name="keep", bufs=1))
         grp = ctx.enter_context(tc.tile_pool(name="grp", bufs=6))
-        tmp = ctx.enter_context(tc.tile_pool(name="tmp", bufs=2))
         stage = ctx.enter_context(tc.tile_pool(name="stage", bufs=6))
-        tp = ctx.enter_context(tc.psum_pool(name="tp", bufs=4))
-        acc = ctx.enter_context(tc.psum_pool(name="acc", bufs=4))
+        tp = ctx.enter_context(tc.psum_pool(name="tp", bufs=TP_BUFS))
+        acc = ctx.enter_context(tc.psum_pool(name="acc", bufs=ACC_BUFS))
 
         ident = const.tile([P, P], F32, name="ident")
         make_identity(nc, ident[:])
@@ -55,274 +87,154 @@ def tile_cp_sparse_degree_lu_pb_kernel(tc, z, chain_lo, U_hi, masks_hi, C_w, C_b
         nc.scalar.dma_start(out=bias_row[0:1, :], in_=C_b.unsqueeze(0))
         bias = const.tile([P, OUTS], F32, name="bias")
 
-        def load_rows(name, rows):
-            t = raw.tile([P, 2, rows.shape[1]], BF16, name=name)
-            nc.sync.dma_start(out=t[:], in_=rows.rearrange("(a p) c -> p a c", p=P))
-            return t
+        loaded = {}
 
-        u_raw = {}
-        m_raw = {}
+        def load(name, view):
+            t = raw.tile([P, 2, view.shape[2]], BF16, name=name)
+            nc.sync.dma_start(out=t[:], in_=view)
+            loaded[name] = t
 
-        def load_factor(i, blk, c0, c1):
-            r0 = 256 * blk - FIRST_RANK
-            m = raw.tile([P, 2, 256], BF16, name="m%d%d" % (i, blk))
-            nc.sync.dma_start(
-                out=m[:],
-                in_=masks_hi[i - 3, r0:r0 + 256, 256 * blk:256 * blk + 256].rearrange("(m e) c -> m e c", e=2))
-            u = raw.tile([P, 2, c1 - c0], BF16, name="u%d%d" % (i, blk))
-            nc.sync.dma_start(out=u[:], in_=U_hi[i - 3, r0:r0 + 256, c0:c1].rearrange("(m e) c -> m e c", e=2))
-            u_raw[(i, blk)] = u
-            m_raw[(i, blk)] = m
+        for name in LOAD_ORDER:
+            if name[:2] == "cw":
+                q = int(name[2])
+                load(name, C_w[256 * q:256 * q + 256, :].rearrange("(a p) c -> p a c", p=P))
+            elif name[0] in "MU":
+                i, blk = int(name[1]), int(name[2])
+                r0 = 256 * blk - FIRST_RANK
+                c0, c1 = ALIVE[(i, blk)] if name[0] == "U" else (256 * blk, 256 * blk + 256)
+                src = U_hi if name[0] == "U" else masks_hi
+                load(name, src[i - 3, r0:r0 + 256, c0:c1].rearrange("(m e) c -> m e c", e=2))
+            else:
+                src = zf if name[0] == "z" else chain_lo
+                pair = int(name[3])
+                c0, c1 = (512, 1536) if name[1:3] == "hi" else (0, 512)
+                load(name, src[256 * pair:256 * pair + 256, c0:c1].rearrange("(a p) c -> p a c", p=P))
 
-        z_raw = {}
-        ch_raw = {}
+        for name in LOAD_ORDER:
+            if name[0] == "U":
+                i, blk = int(name[1]), int(name[2])
+                d0 = 256 * blk - ALIVE[(i, blk)][0]
+                u = loaded[name]
+                nc.gpsimd.tensor_tensor(out=u[:, :, d0:d0 + 256], in0=u[:, :, d0:d0 + 256], in1=loaded["M" + name[1:]][:],
+                                        op=MULT)
 
-        def load_split(store, name, src, part_name, pair):
-            c0, c1 = (512, 1536) if part_name == "hi" else (0, 512)
-            store[(part_name, pair)] = load_rows("%s%s%d" % (name, part_name, pair), src[256 * pair:256 * pair + 256, c0:c1])
+        def words(name, a, first_word):
+            return loaded[name][:].bitcast(F32)[:, a, first_word:first_word + P]
 
-        for pair in range(2):
-            load_split(z_raw, "z", zf, "hi", pair)
-        for pair in range(2):
-            load_split(ch_raw, "ch", chain_lo, "hi", pair)
-        for (i, blk, c0, c1) in FACTOR_BLOCKS[:4]:
-            load_factor(i, blk, c0, c1)
-        for pair in range(2):
-            load_split(z_raw, "z", zf, "lo", pair)
-        for (i, blk, c0, c1) in FACTOR_BLOCKS[4:]:
-            load_factor(i, blk, c0, c1)
-        for pair in range(2):
-            load_split(ch_raw, "ch", chain_lo, "lo", pair)
-        cw_raw = [load_rows("cw%d" % q, C_w[256 * q:256 * q + 256, :]) for q in range(8)]
-
-        for j in range(4):
-            spread = acc.tile([P, 512], F32, name="spread%d" % j, tag="acc")
-            nc.tensor.matmul(out=spread[:], lhsT=ones[:], rhs=bias_row[:, 512 * j:512 * j + 512], start=True, stop=True)
-            nc.scalar.copy(out=bias[:, 512 * j:512 * j + 512], in_=spread[:])
-
-        def transposes(name, sources):
-            bank = tp.tile([P, 2, 2, P], F32, name="tp_" + name, tag="tp")
-            for a in range(2):
-                for u in range(2):
-                    nc.tensor.transpose(bank[:, a, u, :], sources[a][u], ident[:])
-            return bank
-
-        def regroup(bank, grouped):
-            nc.scalar.copy(out=grouped[:].bitcast(F32).rearrange("p (a m u) -> p a m u", a=2, u=2),
-                           in_=bank[:].rearrange("p a u m -> p a m u"))
-
-        def quantise(grouped, codes, scales):
-            nc.vector.quantize_mx(out=codes.bitcast(FP8X4), scales=scales, in_=grouped[:])
-
-        def words(tile_ap, a, first_word):
-            return tile_ap[:].bitcast(F32)[:, a, first_word:first_word + P]
-
-        def row_sources(tile_ap, g):
-            return [[words(tile_ap, a, 256 * g + 128 * u) for u in range(2)] for a in range(2)]
-
-        def split_sources(tiles, pair, g):
-            if g == 0:
-                return row_sources(tiles[("lo", pair)], 0)
-            return row_sources(tiles[("hi", pair)], g - 1)
-
-        zc = {}
-        zs = {}
-        wc = {}
-        ws = {}
-        oc = {}
-        osc = {}
-        cc = {}
-        cs = {}
-        ct = {}
-
-        def z_unit(pair, g):
-            bank = transposes("z%d%d" % (pair, g), split_sources(z_raw, pair, g))
-            grouped = grp.tile([P, 1024], BF16, name="gz%d%d" % (pair, g), tag="grp", align_bytes=64)
-            regroup(bank, grouped)
-            zc[(g, pair)] = keep.tile([P, 256], U32, name="zc%d%d" % (g, pair), align_bytes=64)
-            zs[(g, pair)] = keep.tile([P, 256], U8, name="zs%d%d" % (g, pair), align_bytes=64)
-            return lambda: quantise(grouped, zc[(g, pair)][:], zs[(g, pair)][:])
-
-        def chain_unit(pair, g):
-            bank = transposes("c%d%d" % (pair, g), split_sources(ch_raw, pair, g))
-            ct[(g, pair)] = keep.tile([P, 1024], BF16, name="ct%d%d" % (g, pair), align_bytes=64)
-            regroup(bank, ct[(g, pair)])
-            oc[(g, pair)] = keep.tile([P, 256], U32, name="oc%d%d" % (g, pair), align_bytes=64)
-            osc[(g, pair)] = keep.tile([P, 256], U8, name="os%d%d" % (g, pair), align_bytes=64)
-
-        def chain_quantise(pair, g):
-            quantise(ct[(g, pair)], oc[(g, pair)][:], osc[(g, pair)][:])
-
-        def apply_mask(i, blk, c0):
-            d0 = 256 * blk - c0
-            u = u_raw[(i, blk)]
-            nc.gpsimd.tensor_tensor(out=u[:, :, d0:d0 + 256], in0=u[:, :, d0:d0 + 256], in1=m_raw[(i, blk)][:], op=MULT)
-
-        def factor_unit(i, blk, c0, c1, g):
-            sources = []
+        def sources(unit):
+            d = [int(c) for c in unit[1:]]
+            if unit[0] == "k":
+                return [[words("cw%d" % d[0], a, 256 * d[1] + 128 * u) for u in range(2)] for a in range(2)]
+            if unit[0] in "zc":
+                g, pair = d
+                name = "%s%s%d" % (unit[0], "lo" if g == 0 else "hi", pair)
+                return [[words(name, a, 256 * max(g - 1, 0) + 128 * u) for u in range(2)] for a in range(2)]
+            i, blk, g = d
+            c0, c1 = ALIVE[(i, blk)]
+            res = []
             for e in range(2):
                 row = []
                 for u in range(2):
                     c = 512 * g + 256 * u
-                    if c0 <= c < c1:
-                        row.append(words(u_raw[(i, blk)], e, (c - c0) // 2))
-                    else:
-                        row.append(zero_words[:])
-                sources.append(row)
-            bank = transposes("w%d%d%d" % (i, blk, g), sources)
-            grouped = grp.tile([P, 1024], BF16, name="gw%d%d%d" % (i, blk, g), tag="grp", align_bytes=64)
-            regroup(bank, grouped)
-            wc[(i, blk, g)] = keep.tile([P, 256], U32, name="wc%d%d%d" % (i, blk, g), align_bytes=64)
-            ws[(i, blk, g)] = keep.tile([P, 256], U8, name="ws%d%d%d" % (i, blk, g), align_bytes=64)
-            return lambda: quantise(grouped, wc[(i, blk, g)][:], ws[(i, blk, g)][:])
+                    row.append(words("U%d%d" % (i, blk), e, (c - c0) // 2) if c0 <= c < c1 else zero_words[:])
+                res.append(row)
+            return res
 
-        def cw_unit(q, g):
-            j, h = divmod(q, 2)
-            bank = transposes("cw%d%d" % (q, g), row_sources(cw_raw[q], g))
-            grouped = grp.tile([P, 1024], BF16, name="gc%d%d" % (q, g), tag="grp", align_bytes=64)
-            regroup(bank, grouped)
-            if h == 0:
-                cc[(j, g)] = keep.tile([P, 512], U32, name="cc%d%d" % (j, g), align_bytes=64)
-                cs[(j, g)] = keep.tile([P, 512], U8, name="cs%d%d" % (j, g), align_bytes=64)
-            return lambda: quantise(grouped, cc[(j, g)][:, 256 * h:256 * h + 256], cs[(j, g)][:, 256 * h:256 * h + 256])
+        banks = {}
+        grouped = {}
+        codes = {}
+        scales = {}
+        hi = [keep.tile([P, 256, 2], F32, name="hi%d" % pair) for pair in range(2)]
+        lo = [keep.tile([P, 256, 2], F32, name="lo%d" % pair) for pair in range(2)]
 
-        def factor_bank(i, blk, pair):
-            y = acc.tile([P, 2, 256], F32, name="y%d%d%d" % (i, blk, pair), tag="acc")
-            passes = FACTOR_PASSES[(i, blk)]
-            for e in range(2):
-                for g in passes:
-                    nc.tensor.matmul_mx(
-                        out=y[:, e, :],
-                        lhsT=wc[(i, blk, g)][:, P * e:P * e + P].bitcast(FP8X4),
-                        lhsT_scale=ws[(i, blk, g)][:, P * e:P * e + P],
-                        rhs=zc[(g, pair)][:].bitcast(FP8X4),
-                        rhs_scale=zs[(g, pair)][:],
-                        start=(g == passes[0]),
-                        stop=(g == passes[-1]),
-                    )
-            return y
+        def operand(name, width):
+            codes[name] = keep.tile([P, width], U32, name="q" + name, align_bytes=64)
+            scales[name] = keep.tile([P, width], U8, name="s" + name, align_bytes=64)
+
+        def half(pair, g, u):
+            return grouped["c%d%d" % (g, pair)][:].rearrange("p (n t) -> p n t", t=4)[:, :, 2 * u:2 * u + 2]
 
         def multiply_in(dst, y, src):
             nc.vector.scalar_tensor_tensor(out=dst, in0=y[:].rearrange("p e n -> p n e"), scalar=1.0, in1=src,
                                            op0=ADD, op1=MULT)
 
-        def half(pair, g, u):
-            return ct[(g, pair)][:].rearrange("p (n t) -> p n t", t=4)[:, :, 2 * u:2 * u + 2]
-
-        def project(j, nt):
-            pair, k = divmod(nt, 2)
-            x = acc.tile([P, 512], F32, name="x%d%d" % (j, nt), tag="acc")
-            for g in range(3):
-                nc.tensor.matmul_mx(
-                    out=x[:],
-                    lhsT=oc[(g, pair)][:, P * k:P * k + P].bitcast(FP8X4),
-                    lhsT_scale=osc[(g, pair)][:, P * k:P * k + P],
-                    rhs=cc[(j, g)][:].bitcast(FP8X4),
-                    rhs_scale=cs[(j, g)][:],
-                    start=(g == 0),
-                    stop=(g == 2),
-                )
-            return x
-
-        def finish(j, nt, x):
-            res = stage.tile([P, 512], F32, name="res%d%d" % (j, nt), tag="res")
-            nc.vector.tensor_tensor(out=res[:], in0=x[:], in1=bias[:, 512 * j:512 * j + 512], op=ADD)
-            nc.sync.dma_start(out=of[P * nt:P * nt + P, 512 * j:512 * j + 512], in_=res[:])
-
-
-        FB = {(i, blk): (c0, c1) for (i, blk, c0, c1) in FACTOR_BLOCKS}
-        PAIRS = (0, 1)
-
-        def funit(i, blk, g):
-            return factor_unit(i, blk, FB[(i, blk)][0], FB[(i, blk)][1], g)
-
-        def mask(i, blk):
-            apply_mask(i, blk, FB[(i, blk)][0])
-
-        def banks(i, blk):
-            return [factor_bank(i, blk, pair) for pair in PAIRS]
-
-        hi = [tmp.tile([P, 256, 2], F32, name="hi%d" % pair) for pair in PAIRS]
-        lo = [tmp.tile([P, 256, 2], F32, name="lo%d" % pair) for pair in PAIRS]
-
-        for g in (2, 1):
-            for pair in PAIRS:
-                z_unit(pair, g)()
-        for g in (2, 1):
-            for pair in PAIRS:
-                chain_unit(pair, g)
-        mask(5, 5)
-        mask(3, 5)
-        q55 = funit(5, 5, 2)
-        q35 = funit(3, 5, 2)
-        q55()
-        mask(3, 4)
-        q35()
-        y = banks(5, 5)
-        q34 = funit(3, 4, 2)
-        for pair in PAIRS:
-            multiply_in(hi[pair][:], y[pair], half(pair, 2, 1))
-        mask(3, 3)
-        q34()
-        y = banks(3, 5)
-        q331 = funit(3, 3, 1)
-        q332 = funit(3, 3, 2)
-        for pair in PAIRS:
-            multiply_in(hi[pair][:], y[pair], hi[pair][:])
-        q331()
-        q332()
-        y = banks(3, 4)
-        qz = [z_unit(pair, 0) for pair in PAIRS]
-        for pair in PAIRS:
-            multiply_in(lo[pair][:], y[pair], half(pair, 2, 0))
-        mask(4, 4)
-        y = [factor_bank(3, 3, 0)]
-        q44 = [funit(4, 4, g) for g in range(3)]
-        y.append(factor_bank(3, 3, 1))
-        for q in qz:
-            q()
-        multiply_in(half(0, 1, 1), y[0], half(0, 1, 1))
-        for q in q44:
-            q()
-        multiply_in(half(1, 1, 1), y[1], half(1, 1, 1))
-        mask(4, 5)
-        q45 = [funit(4, 5, g) for g in range(3)]
-        y = [factor_bank(4, 4, 0)]
-        for q in q45:
-            q()
-        for pair in PAIRS:
-            chain_unit(pair, 0)
-        y.append(factor_bank(4, 4, 1))
-        for pair in PAIRS:
-            multiply_in(half(pair, 2, 0), y[pair], lo[pair][:])
-        qc = [cw_unit(0, g) for g in (0, 1)]
-        y = [factor_bank(4, 5, 0)]
-        for pair in PAIRS:
-            chain_quantise(pair, 1)
-            chain_quantise(pair, 0)
-        for q in qc:
-            q()
-        qc = [cw_unit(0, 2), cw_unit(1, 0)]
-        y.append(factor_bank(4, 5, 1))
-        multiply_in(half(0, 2, 1), y[0], hi[0][:])
-        chain_quantise(0, 2)
-        for q in qc:
-            q()
-        multiply_in(half(1, 2, 1), y[1], hi[1][:])
-        chain_quantise(1, 2)
-        qc = [cw_unit(1, g) for g in (1, 2)]
-        for q in qc:
-            q()
-        for step in range(2, 10):
-            qc = []
-            if step < 8:
-                qc = [cw_unit(step, g) for g in range(3)]
-            j, h = divmod(step - 2, 2)
-            for q in qc[:2]:
-                q()
-            for nt in (2 * h, 2 * h + 1):
-                x = project(j, nt)
-                finish(j, nt, x)
-                if nt == 2 * h:
-                    for q in qc[2:]:
-                        q()
+        for (kind, arg) in ORDER:
+            op = kind + ":" + arg
+            if kind == "B":
+                j = int(arg)
+                banks[op] = acc.tile([P, 512], F32, name="spread%d" % j, tag="acc")
+                nc.tensor.matmul(out=banks[op][:], lhsT=ones[:], rhs=bias_row[:, 512 * j:512 * j + 512], start=True,
+                                 stop=True)
+            elif kind == "BC":
+                j = int(arg)
+                nc.scalar.copy(out=bias[:, 512 * j:512 * j + 512], in_=banks["B:" + arg][:])
+            elif kind == "T":
+                banks[arg] = tp.tile([P, 2, 2, P], F32, name="tp_" + arg, tag="tp")
+                src = sources(arg)
+                for a in range(2):
+                    for u in range(2):
+                        nc.tensor.transpose(banks[arg][:, a, u, :], src[a][u], ident[:])
+            elif kind == "C":
+                if arg[0] == "c":
+                    grouped[arg] = keep.tile([P, 1024], BF16, name="g" + arg, align_bytes=64)
+                else:
+                    grouped[arg] = grp.tile([P, 1024], BF16, name="g" + arg, tag="grp", align_bytes=64)
+                nc.scalar.copy(out=grouped[arg][:].bitcast(F32).rearrange("p (a m u) -> p a m u", a=2, u=2),
+                               in_=banks[arg][:].rearrange("p a u m -> p a m u"))
+            elif kind in "QO":
+                if kind == "O":
+                    arg = "c" + arg
+                if arg[0] == "k":
+                    j, h = divmod(int(arg[1]), 2)
+                    name = "k%d%s" % (j, arg[2])
+                    if name not in codes:
+                        operand(name, 512)
+                    dst, dsc = codes[name][:, 256 * h:256 * h + 256], scales[name][:, 256 * h:256 * h + 256]
+                else:
+                    operand(arg, 256)
+                    dst, dsc = codes[arg][:], scales[arg][:]
+                nc.vector.quantize_mx(out=dst.bitcast(FP8X4), scales=dsc, in_=grouped[arg][:])
+            elif kind == "Y":
+                i, blk, pair = int(arg[0]), int(arg[1]), int(arg[2])
+                y = acc.tile([P, 2, 256], F32, name="y" + arg, tag="acc")
+                banks[op] = y
+                passes = PASSES[(i, blk)]
+                for e in range(2):
+                    for g in passes:
+                        w = "w%d%d%d" % (i, blk, g)
+                        zz = "z%d%d" % (g, pair)
+                        nc.tensor.matmul_mx(out=y[:, e, :], lhsT=codes[w][:, P * e:P * e + P].bitcast(FP8X4),
+                                            lhsT_scale=scales[w][:, P * e:P * e + P], rhs=codes[zz][:].bitcast(FP8X4),
+                                            rhs_scale=scales[zz][:], start=(g == passes[0]), stop=(g == passes[-1]))
+            elif kind == "M":
+                pair = int(arg[-1])
+                y = banks["Y:" + arg[-3:]]
+                step = arg[:-1]
+                if step == "hi55":
+                    multiply_in(hi[pair][:], y, half(pair, 2, 1))
+                elif step == "hi35":
+                    multiply_in(hi[pair][:], y, hi[pair][:])
+                elif step == "lo34":
+                    multiply_in(lo[pair][:], y, half(pair, 2, 0))
+                elif step == "o33":
+                    multiply_in(half(pair, 1, 1), y, half(pair, 1, 1))
+                elif step == "o44":
+                    multiply_in(half(pair, 2, 0), y, lo[pair][:])
+                else:
+                    multiply_in(half(pair, 2, 1), y, hi[pair][:])
+            elif kind == "X":
+                j, nt = int(arg[0]), int(arg[1])
+                pair, k = divmod(nt, 2)
+                x = acc.tile([P, 512], F32, name="x" + arg, tag="acc")
+                banks[op] = x
+                for g in range(3):
+                    o = "c%d%d" % (g, pair)
+                    c = "k%d%d" % (j, g)
+                    nc.tensor.matmul_mx(out=x[:], lhsT=codes[o][:, P * k:P * k + P].bitcast(FP8X4),
+                                        lhsT_scale=scales[o][:, P * k:P * k + P], rhs=codes[c][:].bitcast(FP8X4),
+                                        rhs_scale=scales[c][:], start=(g == 0), stop=(g == 2))
+            else:
+                j, nt = int(arg[0]), int(arg[1])
+                res = stage.tile([P, 512], F32, name="res" + arg, tag="res")
+                nc.vector.tensor_tensor(out=res[:], in0=banks["X:" + arg][:], in1=bias[:, 512 * j:512 * j + 512], op=ADD)
+                nc.sync.dma_start(out=of[P * nt:P * nt + P, 512 * j:512 * j + 512], in_=res[:])

@@ -13,52 +13,41 @@ ADD = mybir.AluOpType.add
 MULT = mybir.AluOpType.mult
 
 P = 128
-RANKS = 1536
+PLANE = 256
+K_PASS = 2 * PLANE
+PASSES = 3
+ROW_PAIRS = 2
 OUTS = 2048
+N_TILE = 512
 FIRST_RANK = 768
-
-FLOPS = 2 * 512 * (1441792 + OUTS * RANKS)
-BYTES = 2 * (2 * 512 * 1536 + 36 * 128 * 256 + 12 * 128 * 256 + OUTS * RANKS + OUTS) + 4 * 512 * OUTS
 
 ALIVE = {(5, 5): (1280, 1536), (3, 5): (1280, 1536), (3, 4): (1024, 1536), (3, 3): (768, 1536), (4, 4): (0, 1280),
          (4, 5): (0, 1536)}
-PASSES = {(5, 5): (2,), (3, 5): (2,), (3, 4): (2,), (3, 3): (1, 2), (4, 4): (0, 1, 2), (4, 5): (0, 1, 2)}
-MANUAL = True
-TP_BUFS = 4
-ACC_BUFS = 4
-LOAD_ORDER = (
-    "zhi0", "zhi1", "M55", "U55", "M35", "U35", "M34", "U34", "chi0", "chi1", "M33", "U33", "zlo0", "zlo1", "M44",
-    "U44", "M45", "U45", "clo0", "clo1", "cw0", "cw1", "cw2", "cw3", "cw4", "cw5", "cw6", "cw7",
+FACTOR_BLOCKS = tuple(ALIVE)
+
+FLOPS = 2 * 512 * (1441792 + OUTS * PASSES * K_PASS)
+BYTES = 2 * (2 * 512 * 1536 + (36 + 12) * P * PLANE + OUTS * 1536 + OUTS) + 4 * 512 * OUTS
+
+UNITS = (
+    tuple(("z", g, pair) for pair in range(ROW_PAIRS) for g in (2, 1))
+    + (("w", 5, 5, 2), ("w", 3, 5, 2), ("w", 3, 4, 2))
+    + tuple(("c", g, pair) for pair in range(ROW_PAIRS) for g in (2, 1))
+    + (("w", 3, 3, 1), ("w", 3, 3, 2), ("z", 0, 0), ("z", 0, 1))
+    + tuple(("w", 4, b, g) for b in (4, 5) for g in range(PASSES))
+    + (("c", 0, 0), ("c", 0, 1))
+    + tuple(("k", q, g) for q in range(8) for g in range(PASSES))
 )
-ORDER = (
-    ("T", "z20"), ("T", "z10"), ("C", "z20"), ("T", "z21"), ("C", "z10"), ("Q", "z20"), ("T", "z11"), ("C", "z21"),
-    ("Q", "z10"), ("B", "0"), ("C", "z11"), ("Q", "z21"), ("B", "1"), ("Q", "z11"), ("BC", "0"), ("B", "2"), ("BC",
-    "1"), ("T", "w552"), ("BC", "2"), ("B", "3"), ("C", "w552"), ("T", "w352"), ("BC", "3"), ("T", "w342"), ("Q",
-    "w552"), ("T", "c20"), ("C", "w352"), ("Y", "550"), ("T", "c10"), ("C", "w342"), ("Q", "w352"), ("T", "c21"),
-    ("C", "c20"), ("T", "c11"), ("Y", "551"), ("C", "c10"), ("M", "hi550"), ("Y", "350"), ("C", "c21"), ("Y",
-    "351"), ("Q", "w342"), ("T", "w331"), ("C", "c11"), ("M", "hi551"), ("Y", "340"), ("C", "w331"), ("T", "w332"),
-    ("M", "hi350"), ("T", "z00"), ("Q", "w331"), ("C", "w332"), ("T", "z01"), ("M", "hi351"), ("T", "w440"), ("C",
-    "z00"), ("T", "w441"), ("Q", "w332"), ("Y", "341"), ("C", "z01"), ("Q", "z00"), ("Y", "330"), ("M", "lo340"),
-    ("C", "w440"), ("T", "w442"), ("Q", "z01"), ("C", "w441"), ("M", "lo341"), ("T", "w450"), ("C", "w442"), ("T",
-    "w451"), ("Q", "w440"), ("Y", "331"), ("C", "w450"), ("Q", "w441"), ("Q", "w442"), ("C", "w451"), ("Y", "440"),
-    ("M", "o330"), ("T", "w452"), ("Q", "w450"), ("M", "o331"), ("T", "c00"), ("C", "w452"), ("T", "c01"), ("T",
-    "k00"), ("O", "10"), ("C", "c00"), ("Y", "441"), ("C", "c01"), ("O", "00"), ("Q", "w451"), ("C", "k00"), ("T",
-    "k01"), ("Q", "w452"), ("T", "k02"), ("O", "11"), ("C", "k01"), ("O", "01"), ("T", "k10"), ("Q", "k00"), ("T",
-    "k11"), ("C", "k02"), ("Q", "k01"), ("T", "k12"), ("M", "o440"), ("Y", "450"), ("C", "k10"), ("C", "k11"),
-    ("M", "o441"), ("T", "k20"), ("C", "k12"), ("T", "k21"), ("Q", "k02"), ("C", "k20"), ("T", "k22"), ("Q",
-    "k10"), ("Y", "451"), ("C", "k21"), ("M", "o450"), ("C", "k22"), ("T", "k30"), ("O", "20"), ("T", "k31"), ("Q",
-    "k11"), ("C", "k30"), ("Q", "k12"), ("T", "k32"), ("Q", "k20"), ("T", "k40"), ("C", "k31"), ("Q", "k21"), ("T",
-    "k41"), ("Q", "k22"), ("X", "00"), ("C", "k32"), ("C", "k40"), ("X", "01"), ("C", "k41"), ("E", "00"), ("T",
-    "k42"), ("Q", "k30"), ("Q", "k31"), ("T", "k50"), ("M", "o451"), ("C", "k42"), ("T", "k51"), ("T", "k52"),
-    ("C", "k50"), ("T", "k60"), ("Q", "k32"), ("O", "21"), ("X", "02"), ("C", "k51"), ("Q", "k40"), ("C", "k52"),
-    ("Q", "k41"), ("X", "03"), ("Q", "k42"), ("C", "k60"), ("Q", "k50"), ("E", "01"), ("X", "10"), ("E", "02"),
-    ("X", "11"), ("E", "03"), ("E", "10"), ("X", "12"), ("Q", "k51"), ("E", "11"), ("T", "k61"), ("T", "k62"),
-    ("Q", "k52"), ("C", "k61"), ("T", "k70"), ("E", "12"), ("T", "k71"), ("C", "k62"), ("T", "k72"), ("Q", "k60"),
-    ("X", "13"), ("Q", "k61"), ("C", "k70"), ("Q", "k62"), ("C", "k71"), ("X", "20"), ("C", "k72"), ("E", "13"),
-    ("X", "21"), ("Q", "k70"), ("E", "20"), ("X", "22"), ("E", "21"), ("X", "23"), ("Q", "k71"), ("Q", "k72"),
-    ("E", "22"), ("X", "30"), ("E", "23"), ("X", "31"), ("E", "30"), ("X", "32"), ("E", "31"), ("X", "33"), ("E",
-    "32"), ("E", "33"),
+MATMULS = (
+    tuple(("bias", j) for j in range(4))
+    + tuple(("factor", i, b, pair) for (i, b) in FACTOR_BLOCKS for pair in range(ROW_PAIRS))
+    + tuple(("project", j, nt) for j in range(4) for nt in range(4))
 )
+TENSOR_RUNS = ((4, 3), (1, 1), (4, 1), (2, 2), (2, 2), (4, 2), (3, 1), (3, 2), (4, 1), (4, 1), (5, 4), (5, 4), (6, 8))
+QUANTISE_LAG = 2
+
+
+def label(key):
+    return ("%s" + "_%d" * (len(key) - 1)) % key
 
 
 def tile_cp_sparse_degree_lu_pb_kernel(tc, z, chain_lo, U_hi, masks_hi, C_w, C_b, out):
@@ -66,18 +55,17 @@ def tile_cp_sparse_degree_lu_pb_kernel(tc, z, chain_lo, U_hi, masks_hi, C_w, C_b
     zf = z.flatten_outer_dims()
     of = out.flatten_outer_dims()
     with ExitStack() as ctx:
-        if MANUAL:
-            ctx.enter_context(tc.manual_schedule())
+        ctx.enter_context(tc.manual_schedule())
         const = ctx.enter_context(tc.tile_pool(name="const", bufs=1))
         raw = ctx.enter_context(tc.tile_pool(name="raw", bufs=1))
         keep = ctx.enter_context(tc.tile_pool(name="keep", bufs=1))
-        grp = ctx.enter_context(tc.tile_pool(name="grp", bufs=6))
-        stage = ctx.enter_context(tc.tile_pool(name="stage", bufs=6))
-        tp = ctx.enter_context(tc.psum_pool(name="tp", bufs=TP_BUFS))
-        acc = ctx.enter_context(tc.psum_pool(name="acc", bufs=ACC_BUFS))
+        regrouped = ctx.enter_context(tc.tile_pool(name="regrouped", bufs=6))
+        results = ctx.enter_context(tc.tile_pool(name="results", bufs=6))
+        flipped = ctx.enter_context(tc.psum_pool(name="flipped", bufs=4))
+        sums = ctx.enter_context(tc.psum_pool(name="sums", bufs=4))
 
-        ident = const.tile([P, P], F32, name="ident")
-        make_identity(nc, ident[:])
+        identity = const.tile([P, P], F32, name="identity")
+        make_identity(nc, identity[:])
         zero_words = const.tile([P, P], F32, name="zero_words")
         nc.vector.memset(zero_words[:], 0.0)
         ones = const.tile([P, P], BF16, name="ones")
@@ -89,152 +77,154 @@ def tile_cp_sparse_degree_lu_pb_kernel(tc, z, chain_lo, U_hi, masks_hi, C_w, C_b
 
         loaded = {}
 
-        def load(name, view):
-            t = raw.tile([P, 2, view.shape[2]], BF16, name=name)
-            nc.sync.dma_start(out=t[:], in_=view)
-            loaded[name] = t
+        def load(key, view):
+            loaded[key] = raw.tile([P, 2, view.shape[2]], BF16, name="raw_" + label(key))
+            nc.sync.dma_start(out=loaded[key][:], in_=view)
 
-        for name in LOAD_ORDER:
-            if name[:2] == "cw":
-                q = int(name[2])
-                load(name, C_w[256 * q:256 * q + 256, :].rearrange("(a p) c -> p a c", p=P))
-            elif name[0] in "MU":
-                i, blk = int(name[1]), int(name[2])
-                r0 = 256 * blk - FIRST_RANK
-                c0, c1 = ALIVE[(i, blk)] if name[0] == "U" else (256 * blk, 256 * blk + 256)
-                src = U_hi if name[0] == "U" else masks_hi
-                load(name, src[i - 3, r0:r0 + 256, c0:c1].rearrange("(m e) c -> m e c", e=2))
-            else:
-                src = zf if name[0] == "z" else chain_lo
-                pair = int(name[3])
-                c0, c1 = (512, 1536) if name[1:3] == "hi" else (0, 512)
-                load(name, src[256 * pair:256 * pair + 256, c0:c1].rearrange("(a p) c -> p a c", p=P))
+        def load_rows(name, src, pair, first_pass, end_pass):
+            load((name, pair, first_pass),
+                 src[PLANE * pair:PLANE * (pair + 1), K_PASS * first_pass:K_PASS * end_pass].rearrange(
+                     "(a p) c -> p a c", p=P))
 
-        for name in LOAD_ORDER:
-            if name[0] == "U":
-                i, blk = int(name[1]), int(name[2])
-                d0 = 256 * blk - ALIVE[(i, blk)][0]
-                u = loaded[name]
-                nc.gpsimd.tensor_tensor(out=u[:, :, d0:d0 + 256], in0=u[:, :, d0:d0 + 256], in1=loaded["M" + name[1:]][:],
-                                        op=MULT)
+        def load_factor(i, b):
+            r0 = PLANE * b - FIRST_RANK
+            c0, c1 = ALIVE[(i, b)]
+            rows = slice(r0, r0 + PLANE)
+            load(("m", i, b), masks_hi[i - 3, rows, PLANE * b:PLANE * (b + 1)].rearrange("(m e) c -> m e c", e=2))
+            load(("u", i, b), U_hi[i - 3, rows, c0:c1].rearrange("(m e) c -> m e c", e=2))
 
-        def words(name, a, first_word):
-            return loaded[name][:].bitcast(F32)[:, a, first_word:first_word + P]
+        for pair in range(ROW_PAIRS):
+            load_rows("z", zf, pair, 1, PASSES)
+        for (i, b) in FACTOR_BLOCKS[:3]:
+            load_factor(i, b)
+        for pair in range(ROW_PAIRS):
+            load_rows("c", chain_lo, pair, 1, PASSES)
+        load_factor(*FACTOR_BLOCKS[3])
+        for pair in range(ROW_PAIRS):
+            load_rows("z", zf, pair, 0, 1)
+        for (i, b) in FACTOR_BLOCKS[4:]:
+            load_factor(i, b)
+        for pair in range(ROW_PAIRS):
+            load_rows("c", chain_lo, pair, 0, 1)
+        for q in range(8):
+            load_rows("k", C_w, q, 0, PASSES)
 
-        def sources(unit):
-            d = [int(c) for c in unit[1:]]
-            if unit[0] == "k":
-                return [[words("cw%d" % d[0], a, 256 * d[1] + 128 * u) for u in range(2)] for a in range(2)]
-            if unit[0] in "zc":
-                g, pair = d
-                name = "%s%s%d" % (unit[0], "lo" if g == 0 else "hi", pair)
-                return [[words(name, a, 256 * max(g - 1, 0) + 128 * u) for u in range(2)] for a in range(2)]
-            i, blk, g = d
-            c0, c1 = ALIVE[(i, blk)]
-            res = []
-            for e in range(2):
-                row = []
-                for u in range(2):
-                    c = 512 * g + 256 * u
-                    row.append(words("U%d%d" % (i, blk), e, (c - c0) // 2) if c0 <= c < c1 else zero_words[:])
-                res.append(row)
-            return res
+        for (i, b) in FACTOR_BLOCKS:
+            d0 = PLANE * b - ALIVE[(i, b)][0]
+            triangle = loaded[("u", i, b)][:, :, d0:d0 + PLANE]
+            nc.gpsimd.tensor_tensor(out=triangle, in0=triangle, in1=loaded[("m", i, b)][:], op=MULT)
 
         banks = {}
         grouped = {}
         codes = {}
         scales = {}
-        hi = [keep.tile([P, 256, 2], F32, name="hi%d" % pair) for pair in range(2)]
-        lo = [keep.tile([P, 256, 2], F32, name="lo%d" % pair) for pair in range(2)]
 
-        def operand(name, width):
-            codes[name] = keep.tile([P, width], U32, name="q" + name, align_bytes=64)
-            scales[name] = keep.tile([P, width], U8, name="s" + name, align_bytes=64)
+        def plane_words(unit, a, u):
+            if unit[0] == "w":
+                i, b, g = unit[1:]
+                c0, c1 = ALIVE[(i, b)]
+                c = K_PASS * g + PLANE * u
+                if not c0 <= c < c1:
+                    return zero_words[:]
+                return loaded[("u", i, b)][:].bitcast(F32)[:, a, (c - c0) // 2:(c - c0) // 2 + P]
+            if unit[0] == "k":
+                key, g = ("k", unit[1], 0), unit[2]
+            else:
+                first_pass = min(unit[1], 1)
+                key, g = (unit[0], unit[2], first_pass), unit[1] - first_pass
+            return loaded[key][:].bitcast(F32)[:, a, P * (2 * g + u):P * (2 * g + u + 1)]
 
-        def half(pair, g, u):
-            return grouped["c%d%d" % (g, pair)][:].rearrange("p (n t) -> p n t", t=4)[:, :, 2 * u:2 * u + 2]
+        def transpose_unit(unit):
+            banks[unit] = flipped.tile([P, 2, 2, P], F32, name="flipped_" + label(unit), tag="flipped")
+            for a in range(2):
+                for u in range(2):
+                    nc.tensor.transpose(banks[unit][:, a, u, :], plane_words(unit, a, u), identity[:])
+            if unit[0] == "c":
+                grouped[unit] = keep.tile([P, 4 * PLANE], BF16, name="grouped_" + label(unit), align_bytes=64)
+            else:
+                grouped[unit] = regrouped.tile([P, 4 * PLANE], BF16, name="grouped_" + label(unit), tag="grouped",
+                                               align_bytes=64)
+            nc.scalar.copy(out=grouped[unit][:].bitcast(F32).rearrange("p (a m u) -> p a m u", a=2, u=2),
+                           in_=banks[unit][:].rearrange("p a u m -> p a m u"))
 
-        def multiply_in(dst, y, src):
-            nc.vector.scalar_tensor_tensor(out=dst, in0=y[:].rearrange("p e n -> p n e"), scalar=1.0, in1=src,
-                                           op0=ADD, op1=MULT)
+        def quantise_unit(unit):
+            if unit[0] == "k":
+                operand, first = ("k", unit[1] // 2, unit[2]), PLANE * (unit[1] % 2)
+                width = N_TILE
+            else:
+                operand, first, width = unit, 0, PLANE
+            if operand not in codes:
+                codes[operand] = keep.tile([P, width], U32, name="codes_" + label(operand), align_bytes=64)
+                scales[operand] = keep.tile([P, width], U8, name="scales_" + label(operand), align_bytes=64)
+            nc.vector.quantize_mx(out=codes[operand][:, first:first + PLANE].bitcast(FP8X4),
+                                  scales=scales[operand][:, first:first + PLANE], in_=grouped[unit][:])
 
-        for (kind, arg) in ORDER:
-            op = kind + ":" + arg
-            if kind == "B":
-                j = int(arg)
-                banks[op] = acc.tile([P, 512], F32, name="spread%d" % j, tag="acc")
-                nc.tensor.matmul(out=banks[op][:], lhsT=ones[:], rhs=bias_row[:, 512 * j:512 * j + 512], start=True,
-                                 stop=True)
-            elif kind == "BC":
-                j = int(arg)
-                nc.scalar.copy(out=bias[:, 512 * j:512 * j + 512], in_=banks["B:" + arg][:])
-            elif kind == "T":
-                banks[arg] = tp.tile([P, 2, 2, P], F32, name="tp_" + arg, tag="tp")
-                src = sources(arg)
-                for a in range(2):
-                    for u in range(2):
-                        nc.tensor.transpose(banks[arg][:, a, u, :], src[a][u], ident[:])
-            elif kind == "C":
-                if arg[0] == "c":
-                    grouped[arg] = keep.tile([P, 1024], BF16, name="g" + arg, align_bytes=64)
-                else:
-                    grouped[arg] = grp.tile([P, 1024], BF16, name="g" + arg, tag="grp", align_bytes=64)
-                nc.scalar.copy(out=grouped[arg][:].bitcast(F32).rearrange("p (a m u) -> p a m u", a=2, u=2),
-                               in_=banks[arg][:].rearrange("p a u m -> p a m u"))
-            elif kind in "QO":
-                if kind == "O":
-                    arg = "c" + arg
-                if arg[0] == "k":
-                    j, h = divmod(int(arg[1]), 2)
-                    name = "k%d%s" % (j, arg[2])
-                    if name not in codes:
-                        operand(name, 512)
-                    dst, dsc = codes[name][:, 256 * h:256 * h + 256], scales[name][:, 256 * h:256 * h + 256]
-                else:
-                    operand(arg, 256)
-                    dst, dsc = codes[arg][:], scales[arg][:]
-                nc.vector.quantize_mx(out=dst.bitcast(FP8X4), scales=dsc, in_=grouped[arg][:])
-            elif kind == "Y":
-                i, blk, pair = int(arg[0]), int(arg[1]), int(arg[2])
-                y = acc.tile([P, 2, 256], F32, name="y" + arg, tag="acc")
-                banks[op] = y
-                passes = PASSES[(i, blk)]
+        def mx_pass(acc, stationary, column, moving, start, stop):
+            nc.tensor.matmul_mx(out=acc, lhsT=codes[stationary][:, column:column + P].bitcast(FP8X4),
+                                lhsT_scale=scales[stationary][:, column:column + P],
+                                rhs=codes[moving][:].bitcast(FP8X4), rhs_scale=scales[moving][:], start=start,
+                                stop=stop)
+
+        partial = {(b, pair): keep.tile([P, PLANE, 2], F32, name="partial_%d_%d" % (b, pair))
+                   for b in (4, 5) for pair in range(ROW_PAIRS)}
+        factors_of = {b: [i for (i, bb) in FACTOR_BLOCKS if bb == b] for b in (3, 4, 5)}
+        steps_left = {(g, pair): sum(len(factors_of.get(b, ())) for b in (2 * g, 2 * g + 1))
+                      for g in range(PASSES) for pair in range(ROW_PAIRS)}
+
+        def chain_block(b, pair):
+            whole = grouped[("c", b // 2, pair)][:].rearrange("p (n t) -> p n t", t=4)
+            return whole[:, :, 2 * (b % 2):2 * (b % 2) + 2]
+
+        def multiply_in(i, b, pair):
+            src = chain_block(b, pair) if i == factors_of[b][0] else partial[(b, pair)][:]
+            dst = chain_block(b, pair) if i == factors_of[b][-1] else partial[(b, pair)][:]
+            nc.vector.scalar_tensor_tensor(out=dst, in0=banks[("factor", i, b, pair)][:].rearrange("p e n -> p n e"),
+                                           scalar=1.0, in1=src, op0=ADD, op1=MULT)
+            steps_left[(b // 2, pair)] -= 1
+            if steps_left[(b // 2, pair)] == 0:
+                quantise_unit(("c", b // 2, pair))
+
+        def matmul_job(job):
+            if job[0] == "bias":
+                cols = slice(N_TILE * job[1], N_TILE * (job[1] + 1))
+                banks[job] = sums.tile([P, N_TILE], F32, name=label(job), tag="sums")
+                nc.tensor.matmul(out=banks[job][:], lhsT=ones[:], rhs=bias_row[:, cols], start=True, stop=True)
+                nc.scalar.copy(out=bias[:, cols], in_=banks[job][:])
+            elif job[0] == "factor":
+                i, b, pair = job[1:]
+                c0, c1 = ALIVE[(i, b)]
+                passes = [g for g in range(PASSES) if c0 < K_PASS * (g + 1) and K_PASS * g < c1]
+                banks[job] = sums.tile([P, 2, PLANE], F32, name=label(job), tag="sums")
                 for e in range(2):
                     for g in passes:
-                        w = "w%d%d%d" % (i, blk, g)
-                        zz = "z%d%d" % (g, pair)
-                        nc.tensor.matmul_mx(out=y[:, e, :], lhsT=codes[w][:, P * e:P * e + P].bitcast(FP8X4),
-                                            lhsT_scale=scales[w][:, P * e:P * e + P], rhs=codes[zz][:].bitcast(FP8X4),
-                                            rhs_scale=scales[zz][:], start=(g == passes[0]), stop=(g == passes[-1]))
-            elif kind == "M":
-                pair = int(arg[-1])
-                y = banks["Y:" + arg[-3:]]
-                step = arg[:-1]
-                if step == "hi55":
-                    multiply_in(hi[pair][:], y, half(pair, 2, 1))
-                elif step == "hi35":
-                    multiply_in(hi[pair][:], y, hi[pair][:])
-                elif step == "lo34":
-                    multiply_in(lo[pair][:], y, half(pair, 2, 0))
-                elif step == "o33":
-                    multiply_in(half(pair, 1, 1), y, half(pair, 1, 1))
-                elif step == "o44":
-                    multiply_in(half(pair, 2, 0), y, lo[pair][:])
-                else:
-                    multiply_in(half(pair, 2, 1), y, hi[pair][:])
-            elif kind == "X":
-                j, nt = int(arg[0]), int(arg[1])
-                pair, k = divmod(nt, 2)
-                x = acc.tile([P, 512], F32, name="x" + arg, tag="acc")
-                banks[op] = x
-                for g in range(3):
-                    o = "c%d%d" % (g, pair)
-                    c = "k%d%d" % (j, g)
-                    nc.tensor.matmul_mx(out=x[:], lhsT=codes[o][:, P * k:P * k + P].bitcast(FP8X4),
-                                        lhsT_scale=scales[o][:, P * k:P * k + P], rhs=codes[c][:].bitcast(FP8X4),
-                                        rhs_scale=scales[c][:], start=(g == 0), stop=(g == 2))
+                        mx_pass(banks[job][:, e, :], ("w", i, b, g), P * e, ("z", g, pair), g == passes[0],
+                                g == passes[-1])
+                multiply_in(i, b, pair)
             else:
-                j, nt = int(arg[0]), int(arg[1])
-                res = stage.tile([P, 512], F32, name="res" + arg, tag="res")
-                nc.vector.tensor_tensor(out=res[:], in0=banks["X:" + arg][:], in1=bias[:, 512 * j:512 * j + 512], op=ADD)
-                nc.sync.dma_start(out=of[P * nt:P * nt + P, 512 * j:512 * j + 512], in_=res[:])
+                j, nt = job[1:]
+                cols = slice(N_TILE * j, N_TILE * (j + 1))
+                banks[job] = sums.tile([P, N_TILE], F32, name=label(job), tag="sums")
+                for g in range(PASSES):
+                    mx_pass(banks[job][:], ("c", g, nt // 2), P * (nt % 2), ("k", j, g), g == 0, g == PASSES - 1)
+                result = results.tile([P, N_TILE], F32, name="result_%d_%d" % (j, nt), tag="result")
+                nc.vector.tensor_tensor(out=result[:], in0=banks[job][:], in1=bias[:, cols], op=ADD)
+                nc.sync.dma_start(out=of[P * nt:P * (nt + 1), cols], in_=result[:])
+
+        tensor_jobs = []
+        units_done, matmuls_done = 0, 0
+        for (n_units, n_matmuls) in TENSOR_RUNS:
+            tensor_jobs += UNITS[units_done:units_done + n_units] + MATMULS[matmuls_done:matmuls_done + n_matmuls]
+            units_done += n_units
+            matmuls_done += n_matmuls
+        assert units_done == len(UNITS) and matmuls_done == len(MATMULS)
+        for position in range(len(tensor_jobs) + QUANTISE_LAG):
+            if position >= QUANTISE_LAG:
+                earlier = tensor_jobs[position - QUANTISE_LAG]
+                if earlier[0] in "zwk" or earlier[0] == "c" and earlier[1] == 0:
+                    quantise_unit(earlier)
+            if position < len(tensor_jobs):
+                job = tensor_jobs[position]
+                if job[0] in "zwkc":
+                    transpose_unit(job)
+                else:
+                    matmul_job(job)

@@ -55,7 +55,6 @@ def tile_cp_sparse_degree_lu_pb_kernel(tc, z, chain_lo, U_hi, masks_hi, C_w, C_b
     zf = z.flatten_outer_dims()
     of = out.flatten_outer_dims()
     with ExitStack() as ctx:
-        ctx.enter_context(tc.manual_schedule())
         const = ctx.enter_context(tc.tile_pool(name="const", bufs=1))
         raw = ctx.enter_context(tc.tile_pool(name="raw", bufs=1))
         keep = ctx.enter_context(tc.tile_pool(name="keep", bufs=1))

@@ -16,38 +16,16 @@ P = 128
 PLANE = 256
 K_PASS = 2 * PLANE
 PASSES = 3
-ROW_PAIRS = 2
+PAIR = 2 * P
 OUTS = 2048
 N_TILE = 512
 FIRST_RANK = 768
 
 ALIVE = {(5, 5): (1280, 1536), (3, 5): (1280, 1536), (3, 4): (1024, 1536), (3, 3): (768, 1536), (4, 4): (0, 1280),
          (4, 5): (0, 1536)}
-FACTOR_BLOCKS = tuple(ALIVE)
 
 FLOPS = 2 * 512 * (1441792 + OUTS * PASSES * K_PASS)
 BYTES = 2 * (2 * 512 * 1536 + (36 + 12) * P * PLANE + OUTS * 1536 + OUTS) + 4 * 512 * OUTS
-
-UNITS = (
-    tuple(("z", g, pair) for pair in range(ROW_PAIRS) for g in (2, 1))
-    + (("w", 5, 5, 2), ("w", 3, 5, 2), ("w", 3, 4, 2))
-    + tuple(("c", g, pair) for pair in range(ROW_PAIRS) for g in (2, 1))
-    + (("w", 3, 3, 1), ("w", 3, 3, 2), ("z", 0, 0), ("z", 0, 1))
-    + tuple(("w", 4, b, g) for b in (4, 5) for g in range(PASSES))
-    + (("c", 0, 0), ("c", 0, 1))
-    + tuple(("k", q, g) for q in range(8) for g in range(PASSES))
-)
-MATMULS = (
-    tuple(("bias", j) for j in range(4))
-    + tuple(("factor", i, b, pair) for (i, b) in FACTOR_BLOCKS for pair in range(ROW_PAIRS))
-    + tuple(("project", j, nt) for j in range(4) for nt in range(4))
-)
-TENSOR_RUNS = ((4, 3), (1, 1), (4, 1), (2, 2), (2, 2), (4, 2), (3, 1), (3, 2), (4, 1), (4, 1), (5, 4), (5, 4), (6, 8))
-QUANTISE_LAG = 2
-
-
-def label(key):
-    return ("%s" + "_%d" * (len(key) - 1)) % key
 
 
 def tile_cp_sparse_degree_lu_pb_kernel(tc, z, chain_lo, U_hi, masks_hi, C_w, C_b, out):
@@ -55,6 +33,7 @@ def tile_cp_sparse_degree_lu_pb_kernel(tc, z, chain_lo, U_hi, masks_hi, C_w, C_b
     zf = z.flatten_outer_dims()
     of = out.flatten_outer_dims()
     with ExitStack() as ctx:
+        ctx.enter_context(tc.manual_schedule())
         const = ctx.enter_context(tc.tile_pool(name="const", bufs=1))
         raw = ctx.enter_context(tc.tile_pool(name="raw", bufs=1))
         keep = ctx.enter_context(tc.tile_pool(name="keep", bufs=1))
@@ -74,156 +53,178 @@ def tile_cp_sparse_degree_lu_pb_kernel(tc, z, chain_lo, U_hi, masks_hi, C_w, C_b
         nc.scalar.dma_start(out=bias_row[0:1, :], in_=C_b.unsqueeze(0))
         bias = const.tile([P, OUTS], F32, name="bias")
 
-        loaded = {}
-
-        def load(key, view):
-            loaded[key] = raw.tile([P, 2, view.shape[2]], BF16, name="raw_" + label(key))
-            nc.sync.dma_start(out=loaded[key][:], in_=view)
-
         def load_rows(name, src, pair, first_pass, end_pass):
-            load((name, pair, first_pass),
-                 src[PLANE * pair:PLANE * (pair + 1), K_PASS * first_pass:K_PASS * end_pass].rearrange(
-                     "(a p) c -> p a c", p=P))
+            tile = raw.tile([P, 2, K_PASS * (end_pass - first_pass)], BF16, name="%s_%d_%d" % (name, pair, first_pass))
+            nc.sync.dma_start(out=tile[:], in_=src[PAIR * pair:PAIR * (pair + 1), K_PASS * first_pass:K_PASS * end_pass]
+                              .rearrange("(a p) c -> p a c", p=P))
+            return tile
+
+        weights = {}
+        triangles = {}
 
         def load_factor(i, b):
-            r0 = PLANE * b - FIRST_RANK
+            rows = slice(PLANE * b - FIRST_RANK, PLANE * (b + 1) - FIRST_RANK)
             c0, c1 = ALIVE[(i, b)]
-            rows = slice(r0, r0 + PLANE)
-            load(("m", i, b), masks_hi[i - 3, rows, PLANE * b:PLANE * (b + 1)].rearrange("(m e) c -> m e c", e=2))
-            load(("u", i, b), U_hi[i - 3, rows, c0:c1].rearrange("(m e) c -> m e c", e=2))
+            triangles[(i, b)] = raw.tile([P, 2, PLANE], BF16, name="mask_%d_%d" % (i, b))
+            nc.sync.dma_start(out=triangles[(i, b)][:],
+                              in_=masks_hi[i - 3, rows, PLANE * b:PLANE * (b + 1)].rearrange("(m e) c -> m e c", e=2))
+            weights[(i, b)] = raw.tile([P, 2, c1 - c0], BF16, name="u_%d_%d" % (i, b))
+            nc.sync.dma_start(out=weights[(i, b)][:], in_=U_hi[i - 3, rows, c0:c1].rearrange("(m e) c -> m e c", e=2))
 
-        for pair in range(ROW_PAIRS):
-            load_rows("z", zf, pair, 1, PASSES)
-        for (i, b) in FACTOR_BLOCKS[:3]:
-            load_factor(i, b)
-        for pair in range(ROW_PAIRS):
-            load_rows("c", chain_lo, pair, 1, PASSES)
-        load_factor(*FACTOR_BLOCKS[3])
-        for pair in range(ROW_PAIRS):
-            load_rows("z", zf, pair, 0, 1)
-        for (i, b) in FACTOR_BLOCKS[4:]:
-            load_factor(i, b)
-        for pair in range(ROW_PAIRS):
-            load_rows("c", chain_lo, pair, 0, 1)
-        for q in range(8):
-            load_rows("k", C_w, q, 0, PASSES)
+        z_back = [load_rows("z", zf, pair, 1, PASSES) for pair in range(2)]
+        load_factor(5, 5)
+        chain_back = [load_rows("chain", chain_lo, pair, 1, PASSES) for pair in range(2)]
+        load_factor(3, 5)
+        load_factor(3, 4)
+        load_factor(3, 3)
+        z_front = [load_rows("z", zf, pair, 0, 1) for pair in range(2)]
+        load_factor(4, 4)
+        load_factor(4, 5)
+        chain_front = [load_rows("chain", chain_lo, pair, 0, 1) for pair in range(2)]
+        c_rows = [load_rows("c_w", C_w, q, 0, PASSES) for q in range(OUTS // PAIR)]
 
-        for (i, b) in FACTOR_BLOCKS:
+        for (i, b) in ALIVE:
             d0 = PLANE * b - ALIVE[(i, b)][0]
-            triangle = loaded[("u", i, b)][:, :, d0:d0 + PLANE]
-            nc.gpsimd.tensor_tensor(out=triangle, in0=triangle, in1=loaded[("m", i, b)][:], op=MULT)
+            triangle = weights[(i, b)][:, :, d0:d0 + PLANE]
+            nc.gpsimd.tensor_tensor(out=triangle, in0=triangle, in1=triangles[(i, b)][:], op=MULT)
 
-        banks = {}
-        grouped = {}
-        codes = {}
-        scales = {}
-
-        def plane_words(unit, a, u):
-            if unit[0] == "w":
-                i, b, g = unit[1:]
-                c0, c1 = ALIVE[(i, b)]
-                c = K_PASS * g + PLANE * u
-                if not c0 <= c < c1:
-                    return zero_words[:]
-                return loaded[("u", i, b)][:].bitcast(F32)[:, a, (c - c0) // 2:(c - c0) // 2 + P]
-            if unit[0] == "k":
-                key, g = ("k", unit[1], 0), unit[2]
-            else:
-                first_pass = min(unit[1], 1)
-                key, g = (unit[0], unit[2], first_pass), unit[1] - first_pass
-            return loaded[key][:].bitcast(F32)[:, a, P * (2 * g + u):P * (2 * g + u + 1)]
-
-        def transpose_unit(unit):
-            banks[unit] = flipped.tile([P, 2, 2, P], F32, name="flipped_" + label(unit), tag="flipped")
+        def flip(name, planes, grouped):
+            bank = flipped.tile([P, 2, 2, P], F32, name="flipped_" + name, tag="flipped")
             for a in range(2):
                 for u in range(2):
-                    nc.tensor.transpose(banks[unit][:, a, u, :], plane_words(unit, a, u), identity[:])
-            if unit[0] == "c":
-                grouped[unit] = keep.tile([P, 4 * PLANE], BF16, name="grouped_" + label(unit), align_bytes=64)
-            else:
-                grouped[unit] = regrouped.tile([P, 4 * PLANE], BF16, name="grouped_" + label(unit), tag="grouped",
-                                               align_bytes=64)
-            nc.scalar.copy(out=grouped[unit][:].bitcast(F32).rearrange("p (a m u) -> p a m u", a=2, u=2),
-                           in_=banks[unit][:].rearrange("p a u m -> p a m u"))
+                    nc.tensor.transpose(bank[:, a, u, :], planes[a][u], identity[:])
+            nc.scalar.copy(out=grouped[:].bitcast(F32).rearrange("p (a m u) -> p a m u", a=2, u=2),
+                           in_=bank[:].rearrange("p a u m -> p a m u"))
 
-        def quantise_unit(unit):
-            if unit[0] == "k":
-                operand, first = ("k", unit[1] // 2, unit[2]), PLANE * (unit[1] % 2)
-                width = N_TILE
-            else:
-                operand, first, width = unit, 0, PLANE
-            if operand not in codes:
-                codes[operand] = keep.tile([P, width], U32, name="codes_" + label(operand), align_bytes=64)
-                scales[operand] = keep.tile([P, width], U8, name="scales_" + label(operand), align_bytes=64)
-            nc.vector.quantize_mx(out=codes[operand][:, first:first + PLANE].bitcast(FP8X4),
-                                  scales=scales[operand][:, first:first + PLANE], in_=grouped[unit][:])
+        def row_planes(tile, g):
+            words = tile[:].bitcast(F32)
+            return [[words[:, a, P * (2 * g + u):P * (2 * g + u + 1)] for u in range(2)] for a in range(2)]
+
+        def operand(name, width):
+            return (keep.tile([P, width], U32, name="codes_" + name, align_bytes=64),
+                    keep.tile([P, width], U8, name="scales_" + name, align_bytes=64))
+
+        def quantise(grouped, target, first):
+            nc.vector.quantize_mx(out=target[0][:, first:first + PAIR].bitcast(FP8X4),
+                                  scales=target[1][:, first:first + PAIR], in_=grouped[:])
+
+        def flip_and_quantise(name, planes, target, first):
+            grouped = regrouped.tile([P, 4 * PAIR], BF16, name="grouped_" + name, tag="grouped", align_bytes=64)
+            flip(name, planes, grouped)
+            quantise(grouped, target, first)
+
+        z_mx = {}
+        w_mx = {}
+        chain = {}
+        chain_mx = {}
+        c_mx = {}
+
+        def prepare_z(tiles, first_pass, passes):
+            for pair in range(2):
+                for g in passes:
+                    name = "z_%d_%d" % (g, pair)
+                    z_mx[(g, pair)] = operand(name, PAIR)
+                    flip_and_quantise(name, row_planes(tiles[pair], g - first_pass), z_mx[(g, pair)], 0)
+
+        def prepare_chain(tiles, first_pass, passes):
+            for pair in range(2):
+                for g in passes:
+                    chain[(g, pair)] = keep.tile([P, 4 * PAIR], BF16, name="chain_%d_%d" % (g, pair), align_bytes=64)
+                    chain_mx[(g, pair)] = operand("chain_%d_%d" % (g, pair), PAIR)
+                    flip("chain_%d_%d" % (g, pair), row_planes(tiles[pair], g - first_pass), chain[(g, pair)])
+
+        def passes_of(i, b):
+            c0, c1 = ALIVE[(i, b)]
+            return [g for g in range(PASSES) if c0 < K_PASS * (g + 1) and K_PASS * g < c1]
+
+        def prepare_factor(i, b):
+            c0, c1 = ALIVE[(i, b)]
+            words = weights[(i, b)][:].bitcast(F32)
+            for g in passes_of(i, b):
+                planes = [[words[:, e, (c - c0) // 2:(c - c0) // 2 + P] if c0 <= c < c1 else zero_words[:]
+                           for c in (K_PASS * g, K_PASS * g + PLANE)] for e in range(2)]
+                w_mx[(i, b, g)] = operand("w_%d_%d_%d" % (i, b, g), PAIR)
+                flip_and_quantise("w_%d_%d_%d" % (i, b, g), planes, w_mx[(i, b, g)], 0)
+
+        def prepare_c(q):
+            for g in range(PASSES):
+                if q % 2 == 0:
+                    c_mx[(q // 2, g)] = operand("c_%d_%d" % (q // 2, g), N_TILE)
+                flip_and_quantise("c_%d_%d" % (q, g), row_planes(c_rows[q], g), c_mx[(q // 2, g)], PAIR * (q % 2))
 
         def mx_pass(acc, stationary, column, moving, start, stop):
-            nc.tensor.matmul_mx(out=acc, lhsT=codes[stationary][:, column:column + P].bitcast(FP8X4),
-                                lhsT_scale=scales[stationary][:, column:column + P],
-                                rhs=codes[moving][:].bitcast(FP8X4), rhs_scale=scales[moving][:], start=start,
-                                stop=stop)
+            nc.tensor.matmul_mx(out=acc, lhsT=stationary[0][:, column:column + P].bitcast(FP8X4),
+                                lhsT_scale=stationary[1][:, column:column + P], rhs=moving[0][:].bitcast(FP8X4),
+                                rhs_scale=moving[1][:], start=start, stop=stop)
 
-        partial = {(b, pair): keep.tile([P, PLANE, 2], F32, name="partial_%d_%d" % (b, pair))
-                   for b in (4, 5) for pair in range(ROW_PAIRS)}
-        factors_of = {b: [i for (i, bb) in FACTOR_BLOCKS if bb == b] for b in (3, 4, 5)}
-        steps_left = {(g, pair): sum(len(factors_of.get(b, ())) for b in (2 * g, 2 * g + 1))
-                      for g in range(PASSES) for pair in range(ROW_PAIRS)}
+        def spread_bias():
+            for j in range(OUTS // N_TILE):
+                cols = slice(N_TILE * j, N_TILE * (j + 1))
+                spread = sums.tile([P, N_TILE], F32, name="spread_%d" % j, tag="sums")
+                nc.tensor.matmul(out=spread[:], lhsT=ones[:], rhs=bias_row[:, cols], start=True, stop=True)
+                nc.scalar.copy(out=bias[:, cols], in_=spread[:])
+
+        partial = {(b, pair): keep.tile([P, PAIR, 2], F32, name="partial_%d_%d" % (b, pair))
+                   for b in (4, 5) for pair in range(2)}
 
         def chain_block(b, pair):
-            whole = grouped[("c", b // 2, pair)][:].rearrange("p (n t) -> p n t", t=4)
-            return whole[:, :, 2 * (b % 2):2 * (b % 2) + 2]
+            return chain[(b // 2, pair)][:].rearrange("p (n t) -> p n t", t=4)[:, :, 2 * (b % 2):2 * (b % 2) + 2]
 
-        def multiply_in(i, b, pair):
-            src = chain_block(b, pair) if i == factors_of[b][0] else partial[(b, pair)][:]
-            dst = chain_block(b, pair) if i == factors_of[b][-1] else partial[(b, pair)][:]
-            nc.vector.scalar_tensor_tensor(out=dst, in0=banks[("factor", i, b, pair)][:].rearrange("p e n -> p n e"),
-                                           scalar=1.0, in1=src, op0=ADD, op1=MULT)
-            steps_left[(b // 2, pair)] -= 1
-            if steps_left[(b // 2, pair)] == 0:
-                quantise_unit(("c", b // 2, pair))
-
-        def matmul_job(job):
-            if job[0] == "bias":
-                cols = slice(N_TILE * job[1], N_TILE * (job[1] + 1))
-                banks[job] = sums.tile([P, N_TILE], F32, name=label(job), tag="sums")
-                nc.tensor.matmul(out=banks[job][:], lhsT=ones[:], rhs=bias_row[:, cols], start=True, stop=True)
-                nc.scalar.copy(out=bias[:, cols], in_=banks[job][:])
-            elif job[0] == "factor":
-                i, b, pair = job[1:]
-                c0, c1 = ALIVE[(i, b)]
-                passes = [g for g in range(PASSES) if c0 < K_PASS * (g + 1) and K_PASS * g < c1]
-                banks[job] = sums.tile([P, 2, PLANE], F32, name=label(job), tag="sums")
+        def factor(i, b, first, last, finished_pass):
+            for pair in range(2):
+                y = sums.tile([P, 2, PAIR], F32, name="y_%d_%d_%d" % (i, b, pair), tag="sums")
+                passes = passes_of(i, b)
                 for e in range(2):
                     for g in passes:
-                        mx_pass(banks[job][:, e, :], ("w", i, b, g), P * e, ("z", g, pair), g == passes[0],
-                                g == passes[-1])
-                multiply_in(i, b, pair)
-            else:
-                j, nt = job[1:]
-                cols = slice(N_TILE * j, N_TILE * (j + 1))
-                banks[job] = sums.tile([P, N_TILE], F32, name=label(job), tag="sums")
-                for g in range(PASSES):
-                    mx_pass(banks[job][:], ("c", g, nt // 2), P * (nt % 2), ("k", j, g), g == 0, g == PASSES - 1)
-                result = results.tile([P, N_TILE], F32, name="result_%d_%d" % (j, nt), tag="result")
-                nc.vector.tensor_tensor(out=result[:], in0=banks[job][:], in1=bias[:, cols], op=ADD)
-                nc.sync.dma_start(out=of[P * nt:P * (nt + 1), cols], in_=result[:])
+                        mx_pass(y[:, e, :], w_mx[(i, b, g)], P * e, z_mx[(g, pair)], g == passes[0], g == passes[-1])
+                nc.vector.scalar_tensor_tensor(out=chain_block(b, pair) if last else partial[(b, pair)][:],
+                                               in0=y[:].rearrange("p e n -> p n e"), scalar=1.0,
+                                               in1=chain_block(b, pair) if first else partial[(b, pair)][:],
+                                               op0=ADD, op1=MULT)
+                if finished_pass is not None:
+                    quantise(chain[(finished_pass, pair)], chain_mx[(finished_pass, pair)], 0)
 
-        tensor_jobs = []
-        units_done, matmuls_done = 0, 0
-        for (n_units, n_matmuls) in TENSOR_RUNS:
-            tensor_jobs += UNITS[units_done:units_done + n_units] + MATMULS[matmuls_done:matmuls_done + n_matmuls]
-            units_done += n_units
-            matmuls_done += n_matmuls
-        assert units_done == len(UNITS) and matmuls_done == len(MATMULS)
-        for position in range(len(tensor_jobs) + QUANTISE_LAG):
-            if position >= QUANTISE_LAG:
-                earlier = tensor_jobs[position - QUANTISE_LAG]
-                if earlier[0] in "zwk" or earlier[0] == "c" and earlier[1] == 0:
-                    quantise_unit(earlier)
-            if position < len(tensor_jobs):
-                job = tensor_jobs[position]
-                if job[0] in "zwkc":
-                    transpose_unit(job)
-                else:
-                    matmul_job(job)
+        def project(j, nt):
+            cols = slice(N_TILE * j, N_TILE * (j + 1))
+            x = sums.tile([P, N_TILE], F32, name="x_%d_%d" % (j, nt), tag="sums")
+            for g in range(PASSES):
+                mx_pass(x[:], chain_mx[(g, nt // 2)], P * (nt % 2), c_mx[(j, g)], g == 0, g == PASSES - 1)
+            result = results.tile([P, N_TILE], F32, name="result_%d_%d" % (j, nt), tag="result")
+            nc.vector.tensor_tensor(out=result[:], in0=x[:], in1=bias[:, cols], op=ADD)
+            nc.sync.dma_start(out=of[P * nt:P * (nt + 1), cols], in_=result[:])
+
+        prepare_z(z_back, 1, (2, 1))
+        spread_bias()
+
+        prepare_factor(5, 5)
+        prepare_chain(chain_back, 1, (2, 1))
+
+        prepare_factor(3, 5)
+        factor(5, 5, True, False, None)
+
+        prepare_factor(3, 4)
+        factor(3, 5, False, False, None)
+
+        prepare_factor(3, 3)
+        prepare_z(z_front, 0, (0,))
+        factor(3, 4, True, False, None)
+
+        prepare_factor(4, 4)
+        factor(3, 3, True, True, 1)
+
+        prepare_factor(4, 5)
+        prepare_chain(chain_front, 0, (0,))
+        for pair in range(2):
+            quantise(chain[(0, pair)], chain_mx[(0, pair)], 0)
+        factor(4, 4, False, True, None)
+
+        prepare_c(0)
+        prepare_c(1)
+        factor(4, 5, False, True, 2)
+
+        halves = OUTS // PAIR
+        for q in range(2, halves + 2):
+            if q < halves:
+                prepare_c(q)
+            for nt in (2 * (q % 2), 2 * (q % 2) + 1):
+                project((q - 2) // 2, nt)

@@ -83,10 +83,10 @@ def tile_cp_sparse_degree_lu_pb_kernel(tc, z, chain_lo, U_hi, masks_hi, C_w, C_b
         chain_front = [load_rows("chain", chain_lo, pair, 0, 1) for pair in range(2)]
         c_rows = [load_rows("c_w", C_w, q, 0, PASSES) for q in range(OUTS // PAIR)]
 
-        for (i, b) in ALIVE:
+        def mask_factor(i, b):
             d0 = PLANE * b - ALIVE[(i, b)][0]
             triangle = weights[(i, b)][:, :, d0:d0 + PLANE]
-            nc.gpsimd.tensor_tensor(out=triangle, in0=triangle, in1=triangles[(i, b)][:], op=MULT)
+            nc.vector.tensor_tensor(out=triangle, in0=triangle, in1=triangles[(i, b)][:], op=MULT)
 
         def flip(name, planes, grouped):
             bank = flipped.tile([P, 2, 2, P], F32, name="flipped_" + name, tag="flipped")
@@ -196,20 +196,26 @@ def tile_cp_sparse_degree_lu_pb_kernel(tc, z, chain_lo, U_hi, masks_hi, C_w, C_b
         prepare_z(z_back, 1, (2, 1))
         spread_bias()
 
+        mask_factor(5, 5)
         prepare_factor(5, 5)
+        mask_factor(3, 5)
         prepare_chain(chain_back, 1, (2, 1))
 
         prepare_factor(3, 5)
+        mask_factor(3, 4)
         factor(5, 5, True, False, None)
 
         prepare_factor(3, 4)
+        mask_factor(3, 3)
         factor(3, 5, False, False, None)
 
         prepare_factor(3, 3)
         prepare_z(z_front, 0, (0,))
+        mask_factor(4, 4)
         factor(3, 4, True, False, None)
 
         prepare_factor(4, 4)
+        mask_factor(4, 5)
         factor(3, 3, True, True, 1)
 
         prepare_factor(4, 5)

@@ -18,6 +18,7 @@ K_PASS = 2 * PLANE
 PASSES = 3
 PAIR = 2 * P
 OUTS = 2048
+WARM = 3
 N_TILE = 512
 FIRST_RANK = 768
 
@@ -51,7 +52,9 @@ def tile_cp_sparse_degree_lu_pb_kernel(tc, z, chain_lo, U_hi, masks_hi, C_w, C_b
         bias_row = const.tile([P, OUTS], BF16, name="bias_row")
         nc.vector.memset(bias_row[:].bitcast(I32), 0)
         nc.scalar.dma_start(out=bias_row[0:1, :], in_=C_b.unsqueeze(0))
-        bias = const.tile([P, OUTS], F32, name="bias")
+        warm_rows = const.tile([P, N_TILE], BF16, name="warm_rows")
+        nc.gpsimd.memset(warm_rows[:], 0.0)
+        bias = const.tile([P, OUTS], BF16, name="bias")
 
         def load_rows(name, src, pair, first_pass, end_pass):
             tile = raw.tile([P, 2, K_PASS * (end_pass - first_pass)], BF16, name="%s_%d_%d" % (name, pair, first_pass))
@@ -71,16 +74,25 @@ def tile_cp_sparse_degree_lu_pb_kernel(tc, z, chain_lo, U_hi, masks_hi, C_w, C_b
             weights[(i, b)] = raw.tile([P, 2, c1 - c0], BF16, name="u_%d_%d" % (i, b))
             nc.sync.dma_start(out=weights[(i, b)][:], in_=U_hi[i - 3, rows, c0:c1].rearrange("(m e) c -> m e c", e=2))
 
-        z_back = [load_rows("z", zf, pair, 1, PASSES) for pair in range(2)]
+        z_rows = {}
+        chain_rows = {}
+
+        def load_pass(rows, name, src, g):
+            for pair in range(2):
+                rows[(g, pair)] = load_rows(name, src, pair, g, g + 1)
+
+        load_pass(z_rows, "z", zf, 2)
         load_factor(5, 5)
-        chain_back = [load_rows("chain", chain_lo, pair, 1, PASSES) for pair in range(2)]
         load_factor(3, 5)
+        load_pass(chain_rows, "chain", chain_lo, 2)
         load_factor(3, 4)
+        load_pass(z_rows, "z", zf, 1)
         load_factor(3, 3)
-        z_front = [load_rows("z", zf, pair, 0, 1) for pair in range(2)]
+        load_pass(chain_rows, "chain", chain_lo, 1)
+        load_pass(z_rows, "z", zf, 0)
         load_factor(4, 4)
         load_factor(4, 5)
-        chain_front = [load_rows("chain", chain_lo, pair, 0, 1) for pair in range(2)]
+        load_pass(chain_rows, "chain", chain_lo, 0)
         c_rows = [load_rows("c_w", C_w, q, 0, PASSES) for q in range(OUTS // PAIR)]
 
         def mask_factor(i, b):
@@ -108,61 +120,86 @@ def tile_cp_sparse_degree_lu_pb_kernel(tc, z, chain_lo, U_hi, masks_hi, C_w, C_b
             nc.vector.quantize_mx(out=target[0][:, first:first + PAIR].bitcast(FP8X4),
                                   scales=target[1][:, first:first + PAIR], in_=grouped[:])
 
-        def flip_and_quantise(name, planes, target, first):
-            grouped = regrouped.tile([P, 4 * PAIR], BF16, name="grouped_" + name, tag="grouped", align_bytes=64)
-            flip(name, planes, grouped)
-            quantise(grouped, target, first)
-
         z_mx = {}
         w_mx = {}
         chain = {}
         chain_mx = {}
         c_mx = {}
+        waiting = {}
 
-        def prepare_z(tiles, first_pass, passes):
-            for pair in range(2):
-                for g in passes:
-                    name = "z_%d_%d" % (g, pair)
-                    z_mx[(g, pair)] = operand(name, PAIR)
-                    flip_and_quantise(name, row_planes(tiles[pair], g - first_pass), z_mx[(g, pair)], 0)
+        def flip_next(key, planes):
+            grouped = regrouped.tile([P, 4 * PAIR], BF16, name="grouped_%s_%d_%d_%d" % key, tag="grouped", align_bytes=64)
+            flip("%s_%d_%d_%d" % key, planes, grouped)
+            waiting[key] = grouped
 
-        def prepare_chain(tiles, first_pass, passes):
+        def flip_z(g):
             for pair in range(2):
-                for g in passes:
-                    chain[(g, pair)] = keep.tile([P, 4 * PAIR], BF16, name="chain_%d_%d" % (g, pair), align_bytes=64)
-                    chain_mx[(g, pair)] = operand("chain_%d_%d" % (g, pair), PAIR)
-                    flip("chain_%d_%d" % (g, pair), row_planes(tiles[pair], g - first_pass), chain[(g, pair)])
+                flip_next(("z", g, pair, 0), row_planes(z_rows[(g, pair)], 0))
+
+        def z_op(g, pair):
+            z_mx[(g, pair)] = operand("z_%d_%d" % (g, pair), PAIR)
+            return z_mx[(g, pair)]
+
+        def quantise_z(g):
+            for pair in range(2):
+                quantise(waiting[("z", g, pair, 0)], z_op(g, pair), 0)
+
+        def flip_chain(g):
+            for pair in range(2):
+                name = "chain_%d_%d" % (g, pair)
+                chain[(g, pair)] = keep.tile([P, 4 * PAIR], BF16, name=name, align_bytes=64)
+                chain_mx[(g, pair)] = operand(name, PAIR)
+                flip(name, row_planes(chain_rows[(g, pair)], 0), chain[(g, pair)])
+
+        def quantise_chain(g, pair):
+            quantise(chain[(g, pair)], chain_mx[(g, pair)], 0)
 
         def passes_of(i, b):
             c0, c1 = ALIVE[(i, b)]
             return [g for g in range(PASSES) if c0 < K_PASS * (g + 1) and K_PASS * g < c1]
 
-        def prepare_factor(i, b):
+        def flip_w(i, b):
             c0, c1 = ALIVE[(i, b)]
             words = weights[(i, b)][:].bitcast(F32)
             for g in passes_of(i, b):
                 planes = [[words[:, e, (c - c0) // 2:(c - c0) // 2 + P] if c0 <= c < c1 else zero_words[:]
                            for c in (K_PASS * g, K_PASS * g + PLANE)] for e in range(2)]
-                w_mx[(i, b, g)] = operand("w_%d_%d_%d" % (i, b, g), PAIR)
-                flip_and_quantise("w_%d_%d_%d" % (i, b, g), planes, w_mx[(i, b, g)], 0)
+                flip_next(("w", i, b, g), planes)
 
-        def prepare_c(q):
+        def quantise_w(i, b):
+            for g in passes_of(i, b):
+                w_mx[(i, b, g)] = operand("w_%d_%d_%d" % (i, b, g), PAIR)
+                quantise(waiting[("w", i, b, g)], w_mx[(i, b, g)], 0)
+
+        def flip_c(q):
+            for g in range(PASSES):
+                flip_next(("c", q, g, 0), row_planes(c_rows[q], g))
+
+        def quantise_c(q):
             for g in range(PASSES):
                 if q % 2 == 0:
                     c_mx[(q // 2, g)] = operand("c_%d_%d" % (q // 2, g), N_TILE)
-                flip_and_quantise("c_%d_%d" % (q, g), row_planes(c_rows[q], g), c_mx[(q // 2, g)], PAIR * (q % 2))
+                quantise(waiting[("c", q, g, 0)], c_mx[(q // 2, g)], PAIR * (q % 2))
 
         def mx_pass(acc, stationary, column, moving, start, stop):
             nc.tensor.matmul_mx(out=acc, lhsT=stationary[0][:, column:column + P].bitcast(FP8X4),
                                 lhsT_scale=stationary[1][:, column:column + P], rhs=moving[0][:].bitcast(FP8X4),
                                 rhs_scale=moving[1][:], start=start, stop=stop)
 
-        def spread_bias():
-            for j in range(OUTS // N_TILE):
-                cols = slice(N_TILE * j, N_TILE * (j + 1))
-                spread = sums.tile([P, N_TILE], F32, name="spread_%d" % j, tag="sums")
-                nc.tensor.matmul(out=spread[:], lhsT=ones[:], rhs=bias_row[:, cols], start=True, stop=True)
-                nc.scalar.copy(out=bias[:, cols], in_=spread[:])
+        def warm(n):
+            for j in range(n):
+                dummy = sums.tile([P, N_TILE], F32, name="warm_%d" % j, tag="sums")
+                nc.tensor.matmul(out=dummy[:], lhsT=ones[:], rhs=warm_rows[:], start=True, stop=True)
+
+        def spread_bias(half):
+            spread = sums.tile([P, 2, N_TILE], BF16, name="spread_%d" % half, tag="sums")
+            for j in range(2):
+                nc.tensor.matmul(out=spread[:, j, :], lhsT=ones[:],
+                                 rhs=bias_row[:, N_TILE * (2 * half + j):N_TILE * (2 * half + j + 1)], start=True, stop=True)
+            return spread
+
+        def keep_bias(half, spread):
+            nc.scalar.copy(out=bias[:, 2 * N_TILE * half:2 * N_TILE * (half + 1)].rearrange("p (j n) -> p j n", j=2), in_=spread[:])
 
         partial = {(b, pair): keep.tile([P, PAIR, 2], F32, name="partial_%d_%d" % (b, pair))
                    for b in (4, 5) for pair in range(2)}
@@ -170,67 +207,106 @@ def tile_cp_sparse_degree_lu_pb_kernel(tc, z, chain_lo, U_hi, masks_hi, C_w, C_b
         def chain_block(b, pair):
             return chain[(b // 2, pair)][:].rearrange("p (n t) -> p n t", t=4)[:, :, 2 * (b % 2):2 * (b % 2) + 2]
 
-        def factor(i, b, first, last, finished_pass):
+        ys = {}
+
+        def multiply(i, b):
             for pair in range(2):
                 y = sums.tile([P, 2, PAIR], F32, name="y_%d_%d_%d" % (i, b, pair), tag="sums")
                 passes = passes_of(i, b)
                 for e in range(2):
                     for g in passes:
                         mx_pass(y[:, e, :], w_mx[(i, b, g)], P * e, z_mx[(g, pair)], g == passes[0], g == passes[-1])
-                nc.vector.scalar_tensor_tensor(out=chain_block(b, pair) if last else partial[(b, pair)][:],
-                                               in0=y[:].rearrange("p e n -> p n e"), scalar=1.0,
-                                               in1=chain_block(b, pair) if first else partial[(b, pair)][:],
-                                               op0=ADD, op1=MULT)
-                if finished_pass is not None:
-                    quantise(chain[(finished_pass, pair)], chain_mx[(finished_pass, pair)], 0)
+                ys[(i, b, pair)] = y
+
+        def combine(i, b, pair, first, last):
+            nc.vector.scalar_tensor_tensor(out=chain_block(b, pair) if last else partial[(b, pair)][:],
+                                           in0=ys[(i, b, pair)][:].rearrange("p e n -> p n e"), scalar=1.0,
+                                           in1=chain_block(b, pair) if first else partial[(b, pair)][:],
+                                           op0=ADD, op1=MULT)
+
+        xs = {}
 
         def project(j, nt):
-            cols = slice(N_TILE * j, N_TILE * (j + 1))
             x = sums.tile([P, N_TILE], F32, name="x_%d_%d" % (j, nt), tag="sums")
             for g in range(PASSES):
                 mx_pass(x[:], chain_mx[(g, nt // 2)], P * (nt % 2), c_mx[(j, g)], g == 0, g == PASSES - 1)
+            xs[(j, nt)] = x
+
+        def finish(j, nt):
+            cols = slice(N_TILE * j, N_TILE * (j + 1))
             result = results.tile([P, N_TILE], F32, name="result_%d_%d" % (j, nt), tag="result")
-            nc.vector.tensor_tensor(out=result[:], in0=x[:], in1=bias[:, cols], op=ADD)
+            nc.vector.tensor_tensor(out=result[:], in0=xs[(j, nt)][:], in1=bias[:, cols], op=ADD)
             nc.sync.dma_start(out=of[P * nt:P * (nt + 1), cols], in_=result[:])
 
-        prepare_z(z_back, 1, (2, 1))
-        spread_bias()
-
+        warm(WARM)
+        flip_z(2)
+        quantise(waiting[("z",2,0,0)], z_op(2,0), 0)
         mask_factor(5, 5)
-        prepare_factor(5, 5)
+        quantise(waiting[("z",2,1,0)], z_op(2,1), 0)
+        spread0 = spread_bias(0)
+        flip_w(5, 5)
         mask_factor(3, 5)
-        prepare_chain(chain_back, 1, (2, 1))
-
-        prepare_factor(3, 5)
+        flip_w(3, 5)
+        quantise_w(5, 5)
+        flip_chain(2)
+        multiply(5, 5)
+        quantise_w(3, 5)
         mask_factor(3, 4)
-        factor(5, 5, True, False, None)
-
-        prepare_factor(3, 4)
+        combine(5, 5, 0, True, False)
+        combine(5, 5, 1, True, False)
+        keep_bias(0, spread0)
+        flip_w(3, 4)
+        multiply(3, 5)
+        flip_z(1)
+        combine(3, 5, 0, False, False)
+        quantise_w(3, 4)
+        combine(3, 5, 1, False, False)
+        multiply(3, 4)
         mask_factor(3, 3)
-        factor(3, 5, False, False, None)
-
-        prepare_factor(3, 3)
-        prepare_z(z_front, 0, (0,))
+        quantise_z(1)
+        flip_w(3, 3)
+        flip_chain(1)
+        combine(3, 4, 0, True, False)
+        combine(3, 4, 1, True, False)
+        quantise_w(3, 3)
+        flip_z(0)
+        multiply(3, 3)
         mask_factor(4, 4)
-        factor(3, 4, True, False, None)
-
-        prepare_factor(4, 4)
+        flip_w(4, 4)
+        quantise_z(0)
+        combine(3, 3, 0, True, True)
+        combine(3, 3, 1, True, True)
         mask_factor(4, 5)
-        factor(3, 3, True, True, 1)
-
-        prepare_factor(4, 5)
-        prepare_chain(chain_front, 0, (0,))
-        for pair in range(2):
-            quantise(chain[(0, pair)], chain_mx[(0, pair)], 0)
-        factor(4, 4, False, True, None)
-
-        prepare_c(0)
-        prepare_c(1)
-        factor(4, 5, False, True, 2)
+        quantise_w(4, 4)
+        spread1 = spread_bias(1)
+        flip_w(4, 5)
+        multiply(4, 4)
+        keep_bias(1, spread1)
+        flip_chain(0)
+        quantise_w(4, 5)
+        quantise_chain(1, 0)
+        quantise_chain(1, 1)
+        flip_c(0)
+        combine(4, 4, 0, False, True)
+        combine(4, 4, 1, False, True)
+        multiply(4, 5)
+        quantise_chain(0, 0)
+        quantise_chain(0, 1)
+        quantise_c(0)
+        combine(4, 5, 0, False, True)
+        combine(4, 5, 1, False, True)
+        flip_c(1)
+        quantise_chain(2, 0)
+        quantise_chain(2, 1)
+        quantise_c(1)
 
         halves = OUTS // PAIR
         for q in range(2, halves + 2):
             if q < halves:
-                prepare_c(q)
+                flip_c(q)
             for nt in (2 * (q % 2), 2 * (q % 2) + 1):
                 project((q - 2) // 2, nt)
+            if q < halves:
+                quantise_c(q)
+            for nt in (2 * (q % 2), 2 * (q % 2) + 1):
+                finish((q - 2) // 2, nt)

@@ -177,9 +177,8 @@ def tile_cp_sparse_degree_lu_pb_kernel(tc, z, chain_lo, U_hi, masks_hi, C_w, C_b
 
         def quantise_c(q):
             for g in range(PASSES):
-                if q % 2 == 0:
-                    c_mx[(q // 2, g)] = operand("c_%d_%d" % (q // 2, g), N_TILE)
-                quantise(waiting[("c", q, g, 0)], c_mx[(q // 2, g)], PAIR * (q % 2))
+                c_mx[(q, g)] = operand("c_%d_%d" % (q, g), PAIR)
+                quantise(waiting[("c", q, g, 0)], c_mx[(q, g)], 0)
 
         def mx_pass(acc, stationary, column, moving, start, stop):
             nc.tensor.matmul_mx(out=acc, lhsT=stationary[0][:, column:column + P].bitcast(FP8X4),
@@ -226,17 +225,21 @@ def tile_cp_sparse_degree_lu_pb_kernel(tc, z, chain_lo, U_hi, masks_hi, C_w, C_b
 
         xs = {}
 
-        def project(j, nt):
-            x = sums.tile([P, N_TILE], F32, name="x_%d_%d" % (j, nt), tag="sums")
-            for g in range(PASSES):
-                mx_pass(x[:], chain_mx[(g, nt // 2)], P * (nt % 2), c_mx[(j, g)], g == 0, g == PASSES - 1)
-            xs[(j, nt)] = x
+        def project(q):
+            for pair in range(2):
+                x = sums.tile([P, 2, PAIR], F32, name="x_%d_%d" % (q, pair), tag="sums")
+                for a in range(2):
+                    for g in range(PASSES):
+                        mx_pass(x[:, a, :], chain_mx[(g, pair)], P * a, c_mx[(q, g)], g == 0, g == PASSES - 1)
+                xs[(q, pair)] = x
 
-        def finish(j, nt):
-            cols = slice(N_TILE * j, N_TILE * (j + 1))
-            result = results.tile([P, N_TILE], F32, name="result_%d_%d" % (j, nt), tag="result")
-            nc.vector.tensor_tensor(out=result[:], in0=xs[(j, nt)][:], in1=bias[:, cols], op=ADD)
-            nc.sync.dma_start(out=of[P * nt:P * (nt + 1), cols], in_=result[:])
+        def finish(q):
+            cols = slice(PAIR * q, PAIR * (q + 1))
+            for pair in range(2):
+                result = results.tile([P, 2, PAIR], F32, name="result_%d_%d" % (q, pair), tag="result")
+                nc.vector.tensor_tensor(out=result[:], in0=xs[(q, pair)][:],
+                                        in1=bias[:, cols].unsqueeze(1).to_broadcast([P, 2, PAIR]), op=ADD)
+                nc.sync.dma_start(out=of[PAIR * pair:PAIR * (pair + 1), cols].rearrange("(a p) c -> p a c", p=P), in_=result[:])
 
         warm(WARM)
         flip_z(2)
@@ -301,12 +304,11 @@ def tile_cp_sparse_degree_lu_pb_kernel(tc, z, chain_lo, U_hi, masks_hi, C_w, C_b
         quantise_c(1)
 
         halves = OUTS // PAIR
-        for q in range(2, halves + 2):
-            if q < halves:
-                flip_c(q)
-            for nt in (2 * (q % 2), 2 * (q % 2) + 1):
-                project((q - 2) // 2, nt)
-            if q < halves:
-                quantise_c(q)
-            for nt in (2 * (q % 2), 2 * (q % 2) + 1):
-                finish((q - 2) // 2, nt)
+        for q in range(2, halves):
+            flip_c(q)
+            project(q - 2)
+            quantise_c(q)
+            finish(q - 2)
+        for q in range(halves - 2, halves):
+            project(q)
+            finish(q)

@@ -19,6 +19,9 @@ PASSES = 3
 PAIR = 2 * P
 OUTS = 2048
 WARM = 3
+SUMS = 3
+FLIPS = 5
+VMASK = ((5, 5), (3, 5), (3, 4), (3, 3), (4, 4), (4, 5))
 N_TILE = 512
 FIRST_RANK = 768
 
@@ -40,27 +43,26 @@ def tile_cp_sparse_degree_lu_pb_kernel(tc, z, chain_lo, U_hi, masks_hi, C_w, C_b
         keep = ctx.enter_context(tc.tile_pool(name="keep", bufs=1))
         regrouped = ctx.enter_context(tc.tile_pool(name="regrouped", bufs=6))
         results = ctx.enter_context(tc.tile_pool(name="results", bufs=6))
-        flipped = ctx.enter_context(tc.psum_pool(name="flipped", bufs=4))
-        sums = ctx.enter_context(tc.psum_pool(name="sums", bufs=4))
+        flipped = ctx.enter_context(tc.psum_pool(name="flipped", bufs=FLIPS))
+        sums = ctx.enter_context(tc.psum_pool(name="sums", bufs=SUMS))
 
-        identity = const.tile([P, P], F32, name="identity")
-        make_identity(nc, identity[:])
+        bias_rows = const.tile([P, N_TILE], BF16, name="bias_rows")
+        nc.vector.memset(bias_rows[:].bitcast(I32), 0)
+        nc.scalar.dma_start(out=bias_rows[0:OUTS // N_TILE, :], in_=C_b.rearrange("(j n) -> j n", n=N_TILE))
+        idle_rows = const.tile([P, N_TILE], BF16, name="idle_rows")
+        nc.vector.memset(idle_rows[:].bitcast(I32), 0)
         zero_words = const.tile([P, P], F32, name="zero_words")
         nc.vector.memset(zero_words[:], 0.0)
-        ones = const.tile([P, P], BF16, name="ones")
-        nc.vector.memset(ones[:], 1.0)
-        bias_row = const.tile([P, OUTS], BF16, name="bias_row")
-        nc.vector.memset(bias_row[:].bitcast(I32), 0)
-        nc.scalar.dma_start(out=bias_row[0:1, :], in_=C_b.unsqueeze(0))
-        warm_rows = const.tile([P, N_TILE], BF16, name="warm_rows")
-        nc.gpsimd.memset(warm_rows[:], 0.0)
+        identity = const.tile([P, P], F32, name="identity")
+        make_identity(nc, identity[:])
+        selectors = const.tile([P, P], BF16, name="selectors")
+        nc.gpsimd.tensor_copy(out=selectors[:], in_=identity[:])
         bias = const.tile([P, OUTS], BF16, name="bias")
 
-        def load_rows(name, src, pair, first_pass, end_pass):
-            tile = raw.tile([P, 2, K_PASS * (end_pass - first_pass)], BF16, name="%s_%d_%d" % (name, pair, first_pass))
-            nc.sync.dma_start(out=tile[:], in_=src[PAIR * pair:PAIR * (pair + 1), K_PASS * first_pass:K_PASS * end_pass]
-                              .rearrange("(a p) c -> p a c", p=P))
-            return tile
+        def load_rows(name, src, pair, g0, g1):
+            tile = raw.tile([P, 2, K_PASS * (g1 - g0)], BF16, name="%s_%d_%d" % (name, pair, g0))
+            nc.sync.dma_start(out=tile[:], in_=src[PAIR * pair:PAIR * (pair + 1), K_PASS * g0:K_PASS * g1].rearrange("(p a) c -> p a c", a=2))
+            return {g: (tile, g - g0) for g in range(g0, g1)}
 
         weights = {}
         triangles = {}
@@ -74,31 +76,37 @@ def tile_cp_sparse_degree_lu_pb_kernel(tc, z, chain_lo, U_hi, masks_hi, C_w, C_b
             weights[(i, b)] = raw.tile([P, 2, c1 - c0], BF16, name="u_%d_%d" % (i, b))
             nc.sync.dma_start(out=weights[(i, b)][:], in_=U_hi[i - 3, rows, c0:c1].rearrange("(m e) c -> m e c", e=2))
 
-        z_rows = {}
-        chain_rows = {}
+        z_rows = ({}, {})
+        chain_rows = ({}, {})
+        c_rows = []
 
-        def load_pass(rows, name, src, g):
-            for pair in range(2):
-                rows[(g, pair)] = load_rows(name, src, pair, g, g + 1)
+        def load_z(pair, g0, g1):
+            z_rows[pair].update(load_rows("z", zf, pair, g0, g1))
 
-        load_pass(z_rows, "z", zf, 2)
+        def load_chain(pair, g0, g1):
+            chain_rows[pair].update(load_rows("chain", chain_lo, pair, g0, g1))
+
+        def load_c():
+            c_rows.append(load_rows("c_w", C_w, len(c_rows), 0, PASSES))
+
+        load_z(0, 0, 3)
         load_factor(5, 5)
         load_factor(3, 5)
-        load_pass(chain_rows, "chain", chain_lo, 2)
+        load_chain(0, 0, 3)
         load_factor(3, 4)
-        load_pass(z_rows, "z", zf, 1)
         load_factor(3, 3)
-        load_pass(chain_rows, "chain", chain_lo, 1)
-        load_pass(z_rows, "z", zf, 0)
         load_factor(4, 4)
         load_factor(4, 5)
-        load_pass(chain_rows, "chain", chain_lo, 0)
-        c_rows = [load_rows("c_w", C_w, q, 0, PASSES) for q in range(OUTS // PAIR)]
+        load_z(1, 0, 3)
+        load_chain(1, 0, 3)
+        for q in range(OUTS // PAIR):
+            load_c()
 
         def mask_factor(i, b):
             d0 = PLANE * b - ALIVE[(i, b)][0]
             triangle = weights[(i, b)][:, :, d0:d0 + PLANE]
-            nc.vector.tensor_tensor(out=triangle, in0=triangle, in1=triangles[(i, b)][:], op=MULT)
+            eng = nc.vector if (i, b) in VMASK else nc.gpsimd
+            eng.tensor_tensor(out=triangle, in0=triangle, in1=triangles[(i, b)][:], op=MULT)
 
         def flip(name, planes, grouped):
             bank = flipped.tile([P, 2, 2, P], F32, name="flipped_" + name, tag="flipped")
@@ -108,7 +116,8 @@ def tile_cp_sparse_degree_lu_pb_kernel(tc, z, chain_lo, U_hi, masks_hi, C_w, C_b
             nc.scalar.copy(out=grouped[:].bitcast(F32).rearrange("p (a m u) -> p a m u", a=2, u=2),
                            in_=bank[:].rearrange("p a u m -> p a m u"))
 
-        def row_planes(tile, g):
+        def row_planes(rows, at):
+            tile, g = rows[at]
             words = tile[:].bitcast(F32)
             return [[words[:, a, P * (2 * g + u):P * (2 * g + u + 1)] for u in range(2)] for a in range(2)]
 
@@ -132,24 +141,24 @@ def tile_cp_sparse_degree_lu_pb_kernel(tc, z, chain_lo, U_hi, masks_hi, C_w, C_b
             flip("%s_%d_%d_%d" % key, planes, grouped)
             waiting[key] = grouped
 
-        def flip_z(g):
-            for pair in range(2):
-                flip_next(("z", g, pair, 0), row_planes(z_rows[(g, pair)], 0))
+        def flip_z(pair, gs=(2, 1, 0)):
+            for g in gs:
+                flip_next(("z", g, pair, 0), row_planes(z_rows[pair], g))
 
-        def z_op(g, pair):
-            z_mx[(g, pair)] = operand("z_%d_%d" % (g, pair), PAIR)
-            return z_mx[(g, pair)]
+        def quantise_z(pair, gs=(2, 1, 0)):
+            for g in gs:
+                z_mx[(g, pair)] = operand("z_%d_%d" % (g, pair), PAIR)
+                quantise(waiting[("z", g, pair, 0)], z_mx[(g, pair)], 0)
 
-        def quantise_z(g):
-            for pair in range(2):
-                quantise(waiting[("z", g, pair, 0)], z_op(g, pair), 0)
-
-        def flip_chain(g):
-            for pair in range(2):
+        def flip_chain(pair, gs=(2, 1, 0)):
+            for g in gs:
                 name = "chain_%d_%d" % (g, pair)
                 chain[(g, pair)] = keep.tile([P, 4 * PAIR], BF16, name=name, align_bytes=64)
                 chain_mx[(g, pair)] = operand(name, PAIR)
-                flip(name, row_planes(chain_rows[(g, pair)], 0), chain[(g, pair)])
+                flip(name, row_planes(chain_rows[pair], g), chain[(g, pair)])
+
+        def mask(i, b):
+            mask_factor(i, b)
 
         def quantise_chain(g, pair):
             quantise(chain[(g, pair)], chain_mx[(g, pair)], 0)
@@ -175,8 +184,8 @@ def tile_cp_sparse_degree_lu_pb_kernel(tc, z, chain_lo, U_hi, masks_hi, C_w, C_b
             for g in range(PASSES):
                 flip_next(("c", q, g, 0), row_planes(c_rows[q], g))
 
-        def quantise_c(q):
-            for g in range(PASSES):
+        def quantise_c(q, gs=range(PASSES)):
+            for g in gs:
                 c_mx[(q, g)] = operand("c_%d_%d" % (q, g), PAIR)
                 quantise(waiting[("c", q, g, 0)], c_mx[(q, g)], 0)
 
@@ -187,18 +196,20 @@ def tile_cp_sparse_degree_lu_pb_kernel(tc, z, chain_lo, U_hi, masks_hi, C_w, C_b
 
         def warm(n):
             for j in range(n):
-                dummy = sums.tile([P, N_TILE], F32, name="warm_%d" % j, tag="sums")
-                nc.tensor.matmul(out=dummy[:], lhsT=ones[:], rhs=warm_rows[:], start=True, stop=True)
+                nothing = flipped.tile([P, 2, 2, P], F32, name="nothing_%d" % j, tag="flipped")
+                nc.tensor.matmul(out=nothing[:].rearrange("p a u m -> p (a u m)"), lhsT=idle_rows[:, 0:P], rhs=idle_rows[:], start=True, stop=True)
+
+        spreads = {}
 
         def spread_bias(half):
-            spread = sums.tile([P, 2, N_TILE], BF16, name="spread_%d" % half, tag="sums")
-            for j in range(2):
-                nc.tensor.matmul(out=spread[:, j, :], lhsT=ones[:],
-                                 rhs=bias_row[:, N_TILE * (2 * half + j):N_TILE * (2 * half + j + 1)], start=True, stop=True)
-            return spread
+            spreads[half] = sums.tile([P, 2, N_TILE], BF16, name="spread_%d" % half, tag="sums")
+            for k in range(2):
+                j = 2 * half + k
+                nc.tensor.matmul(out=spreads[half][:, k, :], lhsT=selectors[:, j:j + 1].to_broadcast([P, P]),
+                                 rhs=bias_rows[:], start=True, stop=True)
 
-        def keep_bias(half, spread):
-            nc.scalar.copy(out=bias[:, 2 * N_TILE * half:2 * N_TILE * (half + 1)].rearrange("p (j n) -> p j n", j=2), in_=spread[:])
+        def keep_bias(half):
+            nc.scalar.copy(out=bias[:, 2 * N_TILE * half:2 * N_TILE * (half + 1)].rearrange("p (j n) -> p j n", j=2), in_=spreads[half][:])
 
         partial = {(b, pair): keep.tile([P, PAIR, 2], F32, name="partial_%d_%d" % (b, pair))
                    for b in (4, 5) for pair in range(2)}
@@ -208,14 +219,13 @@ def tile_cp_sparse_degree_lu_pb_kernel(tc, z, chain_lo, U_hi, masks_hi, C_w, C_b
 
         ys = {}
 
-        def multiply(i, b):
-            for pair in range(2):
-                y = sums.tile([P, 2, PAIR], F32, name="y_%d_%d_%d" % (i, b, pair), tag="sums")
-                passes = passes_of(i, b)
-                for e in range(2):
-                    for g in passes:
-                        mx_pass(y[:, e, :], w_mx[(i, b, g)], P * e, z_mx[(g, pair)], g == passes[0], g == passes[-1])
-                ys[(i, b, pair)] = y
+        def multiply(i, b, pair):
+            y = sums.tile([P, 2, PAIR], F32, name="y_%d_%d_%d" % (i, b, pair), tag="sums")
+            passes = passes_of(i, b)
+            for e in range(2):
+                for g in passes:
+                    mx_pass(y[:, e, :], w_mx[(i, b, g)], P * e, z_mx[(g, pair)], g == passes[0], g == passes[-1])
+            ys[(i, b, pair)] = y
 
         def combine(i, b, pair, first, last):
             nc.vector.scalar_tensor_tensor(out=chain_block(b, pair) if last else partial[(b, pair)][:],
@@ -225,90 +235,128 @@ def tile_cp_sparse_degree_lu_pb_kernel(tc, z, chain_lo, U_hi, masks_hi, C_w, C_b
 
         xs = {}
 
-        def project(q):
-            for pair in range(2):
-                x = sums.tile([P, 2, PAIR], F32, name="x_%d_%d" % (q, pair), tag="sums")
-                for a in range(2):
-                    for g in range(PASSES):
-                        mx_pass(x[:, a, :], chain_mx[(g, pair)], P * a, c_mx[(q, g)], g == 0, g == PASSES - 1)
-                xs[(q, pair)] = x
+        def project(q, pair):
+            x = sums.tile([P, 2, PAIR], F32, name="x_%d_%d" % (q, pair), tag="sums")
+            for a in range(2):
+                for g in range(PASSES):
+                    mx_pass(x[:, a, :], chain_mx[(g, pair)], P * a, c_mx[(q, g)], g == 0, g == PASSES - 1)
+            xs[(q, pair)] = x
 
-        def finish(q):
+        def finish(q, pair):
             cols = slice(PAIR * q, PAIR * (q + 1))
-            for pair in range(2):
+            for pair in (pair,):
                 result = results.tile([P, 2, PAIR], F32, name="result_%d_%d" % (q, pair), tag="result")
-                nc.vector.tensor_tensor(out=result[:], in0=xs[(q, pair)][:],
-                                        in1=bias[:, cols].unsqueeze(1).to_broadcast([P, 2, PAIR]), op=ADD)
-                nc.sync.dma_start(out=of[PAIR * pair:PAIR * (pair + 1), cols].rearrange("(a p) c -> p a c", p=P), in_=result[:])
+                nc.vector.tensor_tensor(out=result[:].rearrange("p a (m c) -> p a m c", c=2),
+                                        in0=xs[(q, pair)][:].rearrange("p a (c m) -> p a m c", c=2),
+                                        in1=bias[:, cols].unsqueeze(1).to_broadcast([P, 2, PAIR]).rearrange("p a (m c) -> p a m c", c=2), op=ADD)
+                nc.sync.dma_start(out=of[PAIR * pair:PAIR * (pair + 1), cols].rearrange("(p a) c -> p a c", a=2), in_=result[:])
 
         warm(WARM)
-        flip_z(2)
-        quantise(waiting[("z",2,0,0)], z_op(2,0), 0)
-        mask_factor(5, 5)
-        quantise(waiting[("z",2,1,0)], z_op(2,1), 0)
-        spread0 = spread_bias(0)
+        flip_z(0, (2, 1, 0))
+        mask(5, 5)
+        quantise_z(0, (2,))
+        mask(3, 5)
         flip_w(5, 5)
-        mask_factor(3, 5)
+        quantise_z(0, (1, 0))
         flip_w(3, 5)
+        spread_bias(0)
         quantise_w(5, 5)
-        flip_chain(2)
-        multiply(5, 5)
+        flip_chain(0, (2, 1))
         quantise_w(3, 5)
-        mask_factor(3, 4)
-        combine(5, 5, 0, True, False)
-        combine(5, 5, 1, True, False)
-        keep_bias(0, spread0)
+        keep_bias(0)
+        multiply(5, 5, 0)
+        multiply(3, 5, 0)
+        mask(3, 4)
         flip_w(3, 4)
-        multiply(3, 5)
-        flip_z(1)
+        combine(5, 5, 0, True, False)
+        mask(3, 3)
+        warm(2)
+        flip_w(3, 3)
         combine(3, 5, 0, False, False)
         quantise_w(3, 4)
-        combine(3, 5, 1, False, False)
-        multiply(3, 4)
-        mask_factor(3, 3)
-        quantise_z(1)
-        flip_w(3, 3)
-        flip_chain(1)
-        combine(3, 4, 0, True, False)
-        combine(3, 4, 1, True, False)
+        multiply(3, 4, 0)
+        flip_chain(0, (0,))
         quantise_w(3, 3)
-        flip_z(0)
-        multiply(3, 3)
-        mask_factor(4, 4)
+        mask(4, 4)
+        combine(3, 4, 0, True, False)
         flip_w(4, 4)
-        quantise_z(0)
+        multiply(3, 3, 0)
+        quantise_chain(0, 0)
+        mask(4, 5)
         combine(3, 3, 0, True, True)
-        combine(3, 3, 1, True, True)
-        mask_factor(4, 5)
         quantise_w(4, 4)
-        spread1 = spread_bias(1)
         flip_w(4, 5)
-        multiply(4, 4)
-        keep_bias(1, spread1)
-        flip_chain(0)
+        spread_bias(1)
+        flip_z(1, (2, 1, 0))
         quantise_w(4, 5)
         quantise_chain(1, 0)
-        quantise_chain(1, 1)
-        flip_c(0)
+        multiply(4, 4, 0)
+        multiply(4, 5, 0)
+        quantise_z(1, (2, 1, 0))
         combine(4, 4, 0, False, True)
-        combine(4, 4, 1, False, True)
-        multiply(4, 5)
-        quantise_chain(0, 0)
-        quantise_chain(0, 1)
-        quantise_c(0)
+        keep_bias(1)
+        flip_chain(1, (2, 1))
         combine(4, 5, 0, False, True)
-        combine(4, 5, 1, False, True)
-        flip_c(1)
+        flip_c(0)
+        multiply(5, 5, 1)
+        multiply(3, 5, 1)
+        multiply(3, 4, 1)
+        multiply(3, 3, 1)
         quantise_chain(2, 0)
-        quantise_chain(2, 1)
+        combine(5, 5, 1, True, False)
+        quantise_c(0)
+        combine(3, 5, 1, False, False)
+        combine(3, 4, 1, True, False)
+        combine(3, 3, 1, True, True)
+        flip_chain(1, (0,))
+        flip_c(1)
+        multiply(4, 4, 1)
+        multiply(4, 5, 1)
+        project(0, 0)
+        combine(4, 4, 1, False, True)
         quantise_c(1)
-
+        combine(4, 5, 1, False, True)
+        flip_c(2)
+        quantise_chain(1, 1)
+        quantise_chain(0, 1)
+        project(1, 0)
+        quantise_chain(2, 1)
+        finish(0, 0)
+        quantise_c(2)
+        finish(1, 0)
+        project(0, 1)
+        project(1, 1)
+        finish(0, 1)
+        finish(1, 1)
         halves = OUTS // PAIR
-        for q in range(2, halves):
-            flip_c(q)
-            project(q - 2)
-            quantise_c(q)
-            finish(q - 2)
-        for q in range(halves - 2, halves):
-            project(q)
-            finish(q)
+        flip_c(3)
+        flip_c(4)
+        project(2, 0)
+        project(2, 1)
+        quantise_c(3)
+        finish(2, 0)
+        finish(2, 1)
+        quantise_c(4)
+        flip_c(5)
+        flip_c(6)
+        for r in (3, 4):
+            for pair in range(2):
+                project(r, pair)
+        quantise_c(5)
+        finish(3, 0)
+        finish(3, 1)
+        quantise_c(6)
+        finish(4, 0)
+        finish(4, 1)
+        flip_c(7)
+        for r in (5, 6):
+            for pair in range(2):
+                project(r, pair)
+        quantise_c(7)
+        finish(5, 0)
+        finish(5, 1)
+        finish(6, 0)
+        finish(6, 1)
+        for pair in range(2):
+            project(7, pair)
+            finish(7, pair)

from contextlib import ExitStack

import concourse.mybir as mybir
from concourse.masks import make_identity

F32 = mybir.dt.float32
BF16 = mybir.dt.bfloat16
U32 = mybir.dt.uint32
U8 = mybir.dt.uint8
I32 = mybir.dt.int32
FP8X4 = mybir.dt.float8_e4m3fn_x4
ADD = mybir.AluOpType.add
MULT = mybir.AluOpType.mult

P = 128
PLANE = 256
K_PASS = 2 * PLANE
PASSES = 3
PAIR = 2 * P
OUTS = 2048
WARM = 3
SUMS = 3
FLIPS = 5
VMASK = ((5, 5), (3, 5), (3, 4), (3, 3), (4, 4), (4, 5))
N_TILE = 512
FIRST_RANK = 768

ALIVE = {(5, 5): (1280, 1536), (3, 5): (1280, 1536), (3, 4): (1024, 1536), (3, 3): (768, 1536), (4, 4): (0, 1280),
         (4, 5): (0, 1536)}

FLOPS = 2 * 512 * (1441792 + OUTS * PASSES * K_PASS)
BYTES = 2 * (2 * 512 * 1536 + (36 + 12) * P * PLANE + OUTS * 1536 + OUTS) + 4 * 512 * OUTS


def tile_cp_sparse_degree_lu_pb_kernel(tc, z, chain_lo, U_hi, masks_hi, C_w, C_b, out):
    nc = tc.nc
    zf = z.flatten_outer_dims()
    of = out.flatten_outer_dims()
    with ExitStack() as ctx:
        ctx.enter_context(tc.manual_schedule())
        const = ctx.enter_context(tc.tile_pool(name="const", bufs=1))
        raw = ctx.enter_context(tc.tile_pool(name="raw", bufs=1))
        keep = ctx.enter_context(tc.tile_pool(name="keep", bufs=1))
        regrouped = ctx.enter_context(tc.tile_pool(name="regrouped", bufs=6))
        results = ctx.enter_context(tc.tile_pool(name="results", bufs=6))
        flipped = ctx.enter_context(tc.psum_pool(name="flipped", bufs=FLIPS))
        sums = ctx.enter_context(tc.psum_pool(name="sums", bufs=SUMS))

        bias_rows = const.tile([P, N_TILE], BF16, name="bias_rows")
        nc.vector.memset(bias_rows[:].bitcast(I32), 0)
        nc.scalar.dma_start(out=bias_rows[0:OUTS // N_TILE, :], in_=C_b.rearrange("(j n) -> j n", n=N_TILE))
        idle_rows = const.tile([P, N_TILE], BF16, name="idle_rows")
        nc.vector.memset(idle_rows[:].bitcast(I32), 0)
        zero_words = const.tile([P, P], F32, name="zero_words")
        nc.vector.memset(zero_words[:], 0.0)
        identity = const.tile([P, P], F32, name="identity")
        make_identity(nc, identity[:])
        selectors = const.tile([P, P], BF16, name="selectors")
        nc.gpsimd.tensor_copy(out=selectors[:], in_=identity[:])
        bias = const.tile([P, OUTS], BF16, name="bias")

        def load_rows(name, src, pair, g0, g1):
            tile = raw.tile([P, 2, K_PASS * (g1 - g0)], BF16, name="%s_%d_%d" % (name, pair, g0))
            nc.sync.dma_start(out=tile[:], in_=src[PAIR * pair:PAIR * (pair + 1), K_PASS * g0:K_PASS * g1].rearrange("(p a) c -> p a c", a=2))
            return {g: (tile, g - g0) for g in range(g0, g1)}

        weights = {}
        triangles = {}

        def load_factor(i, b):
            rows = slice(PLANE * b - FIRST_RANK, PLANE * (b + 1) - FIRST_RANK)
            c0, c1 = ALIVE[(i, b)]
            triangles[(i, b)] = raw.tile([P, 2, PLANE], BF16, name="mask_%d_%d" % (i, b))
            nc.sync.dma_start(out=triangles[(i, b)][:],
                              in_=masks_hi[i - 3, rows, PLANE * b:PLANE * (b + 1)].rearrange("(m e) c -> m e c", e=2))
            weights[(i, b)] = raw.tile([P, 2, c1 - c0], BF16, name="u_%d_%d" % (i, b))
            nc.sync.dma_start(out=weights[(i, b)][:], in_=U_hi[i - 3, rows, c0:c1].rearrange("(m e) c -> m e c", e=2))

        z_rows = ({}, {})
        chain_rows = ({}, {})
        c_rows = []

        def load_z(pair, g0, g1):
            z_rows[pair].update(load_rows("z", zf, pair, g0, g1))

        def load_chain(pair, g0, g1):
            chain_rows[pair].update(load_rows("chain", chain_lo, pair, g0, g1))

        def load_c():
            c_rows.append(load_rows("c_w", C_w, len(c_rows), 0, PASSES))

        load_z(0, 0, 3)
        load_factor(5, 5)
        load_factor(3, 5)
        load_chain(0, 0, 3)
        load_factor(3, 4)
        load_factor(3, 3)
        load_factor(4, 4)
        load_factor(4, 5)
        load_z(1, 0, 3)
        load_chain(1, 0, 3)
        for q in range(OUTS // PAIR):
            load_c()

        def mask_factor(i, b):
            d0 = PLANE * b - ALIVE[(i, b)][0]
            triangle = weights[(i, b)][:, :, d0:d0 + PLANE]
            eng = nc.vector if (i, b) in VMASK else nc.gpsimd
            eng.tensor_tensor(out=triangle, in0=triangle, in1=triangles[(i, b)][:], op=MULT)

        def flip(name, planes, grouped):
            bank = flipped.tile([P, 2, 2, P], F32, name="flipped_" + name, tag="flipped")
            for a in range(2):
                for u in range(2):
                    nc.tensor.transpose(bank[:, a, u, :], planes[a][u], identity[:])
            nc.scalar.copy(out=grouped[:].bitcast(F32).rearrange("p (a m u) -> p a m u", a=2, u=2),
                           in_=bank[:].rearrange("p a u m -> p a m u"))

        def row_planes(rows, at):
            tile, g = rows[at]
            words = tile[:].bitcast(F32)
            return [[words[:, a, P * (2 * g + u):P * (2 * g + u + 1)] for u in range(2)] for a in range(2)]

        def operand(name, width):
            return (keep.tile([P, width], U32, name="codes_" + name, align_bytes=64),
                    keep.tile([P, width], U8, name="scales_" + name, align_bytes=64))

        def quantise(grouped, target, first):
            nc.vector.quantize_mx(out=target[0][:, first:first + PAIR].bitcast(FP8X4),
                                  scales=target[1][:, first:first + PAIR], in_=grouped[:])

        z_mx = {}
        w_mx = {}
        chain = {}
        chain_mx = {}
        c_mx = {}
        waiting = {}

        def flip_next(key, planes):
            grouped = regrouped.tile([P, 4 * PAIR], BF16, name="grouped_%s_%d_%d_%d" % key, tag="grouped", align_bytes=64)
            flip("%s_%d_%d_%d" % key, planes, grouped)
            waiting[key] = grouped

        def flip_z(pair, gs=(2, 1, 0)):
            for g in gs:
                flip_next(("z", g, pair, 0), row_planes(z_rows[pair], g))

        def quantise_z(pair, gs=(2, 1, 0)):
            for g in gs:
                z_mx[(g, pair)] = operand("z_%d_%d" % (g, pair), PAIR)
                quantise(waiting[("z", g, pair, 0)], z_mx[(g, pair)], 0)

        def flip_chain(pair, gs=(2, 1, 0)):
            for g in gs:
                name = "chain_%d_%d" % (g, pair)
                chain[(g, pair)] = keep.tile([P, 4 * PAIR], BF16, name=name, align_bytes=64)
                chain_mx[(g, pair)] = operand(name, PAIR)
                flip(name, row_planes(chain_rows[pair], g), chain[(g, pair)])

        def mask(i, b):
            mask_factor(i, b)

        def quantise_chain(g, pair):
            quantise(chain[(g, pair)], chain_mx[(g, pair)], 0)

        def passes_of(i, b):
            c0, c1 = ALIVE[(i, b)]
            return [g for g in range(PASSES) if c0 < K_PASS * (g + 1) and K_PASS * g < c1]

        def flip_w(i, b):
            c0, c1 = ALIVE[(i, b)]
            words = weights[(i, b)][:].bitcast(F32)
            for g in passes_of(i, b):
                planes = [[words[:, e, (c - c0) // 2:(c - c0) // 2 + P] if c0 <= c < c1 else zero_words[:]
                           for c in (K_PASS * g, K_PASS * g + PLANE)] for e in range(2)]
                flip_next(("w", i, b, g), planes)

        def quantise_w(i, b):
            for g in passes_of(i, b):
                w_mx[(i, b, g)] = operand("w_%d_%d_%d" % (i, b, g), PAIR)
                quantise(waiting[("w", i, b, g)], w_mx[(i, b, g)], 0)

        def flip_c(q):
            for g in range(PASSES):
                flip_next(("c", q, g, 0), row_planes(c_rows[q], g))

        def quantise_c(q, gs=range(PASSES)):
            for g in gs:
                c_mx[(q, g)] = operand("c_%d_%d" % (q, g), PAIR)
                quantise(waiting[("c", q, g, 0)], c_mx[(q, g)], 0)

        def mx_pass(acc, stationary, column, moving, start, stop):
            nc.tensor.matmul_mx(out=acc, lhsT=stationary[0][:, column:column + P].bitcast(FP8X4),
                                lhsT_scale=stationary[1][:, column:column + P], rhs=moving[0][:].bitcast(FP8X4),
                                rhs_scale=moving[1][:], start=start, stop=stop)

        def warm(n):
            for j in range(n):
                nothing = flipped.tile([P, 2, 2, P], F32, name="nothing_%d" % j, tag="flipped")
                nc.tensor.matmul(out=nothing[:].rearrange("p a u m -> p (a u m)"), lhsT=idle_rows[:, 0:P], rhs=idle_rows[:], start=True, stop=True)

        spreads = {}

        def spread_bias(half):
            spreads[half] = sums.tile([P, 2, N_TILE], BF16, name="spread_%d" % half, tag="sums")
            for k in range(2):
                j = 2 * half + k
                nc.tensor.matmul(out=spreads[half][:, k, :], lhsT=selectors[:, j:j + 1].to_broadcast([P, P]),
                                 rhs=bias_rows[:], start=True, stop=True)

        def keep_bias(half):
            nc.scalar.copy(out=bias[:, 2 * N_TILE * half:2 * N_TILE * (half + 1)].rearrange("p (j n) -> p j n", j=2), in_=spreads[half][:])

        partial = {(b, pair): keep.tile([P, PAIR, 2], F32, name="partial_%d_%d" % (b, pair))
                   for b in (4, 5) for pair in range(2)}

        def chain_block(b, pair):
            return chain[(b // 2, pair)][:].rearrange("p (n t) -> p n t", t=4)[:, :, 2 * (b % 2):2 * (b % 2) + 2]

        ys = {}

        def multiply(i, b, pair):
            y = sums.tile([P, 2, PAIR], F32, name="y_%d_%d_%d" % (i, b, pair), tag="sums")
            passes = passes_of(i, b)
            for e in range(2):
                for g in passes:
                    mx_pass(y[:, e, :], w_mx[(i, b, g)], P * e, z_mx[(g, pair)], g == passes[0], g == passes[-1])
            ys[(i, b, pair)] = y

        def combine(i, b, pair, first, last):
            nc.vector.scalar_tensor_tensor(out=chain_block(b, pair) if last else partial[(b, pair)][:],
                                           in0=ys[(i, b, pair)][:].rearrange("p e n -> p n e"), scalar=1.0,
                                           in1=chain_block(b, pair) if first else partial[(b, pair)][:],
                                           op0=ADD, op1=MULT)

        xs = {}

        def project(q, pair):
            x = sums.tile([P, 2, PAIR], F32, name="x_%d_%d" % (q, pair), tag="sums")
            for a in range(2):
                for g in range(PASSES):
                    mx_pass(x[:, a, :], chain_mx[(g, pair)], P * a, c_mx[(q, g)], g == 0, g == PASSES - 1)
            xs[(q, pair)] = x

        def finish(q, pair):
            cols = slice(PAIR * q, PAIR * (q + 1))
            for pair in (pair,):
                result = results.tile([P, 2, PAIR], F32, name="result_%d_%d" % (q, pair), tag="result")
                nc.vector.tensor_tensor(out=result[:].rearrange("p a (m c) -> p a m c", c=2),
                                        in0=xs[(q, pair)][:].rearrange("p a (c m) -> p a m c", c=2),
                                        in1=bias[:, cols].unsqueeze(1).to_broadcast([P, 2, PAIR]).rearrange("p a (m c) -> p a m c", c=2), op=ADD)
                nc.sync.dma_start(out=of[PAIR * pair:PAIR * (pair + 1), cols].rearrange("(p a) c -> p a c", a=2), in_=result[:])

        warm(WARM)
        flip_z(0, (2, 1, 0))
        mask(5, 5)
        quantise_z(0, (2,))
        mask(3, 5)
        flip_w(5, 5)
        quantise_z(0, (1, 0))
        flip_w(3, 5)
        spread_bias(0)
        quantise_w(5, 5)
        flip_chain(0, (2, 1))
        quantise_w(3, 5)
        keep_bias(0)
        multiply(5, 5, 0)
        multiply(3, 5, 0)
        mask(3, 4)
        flip_w(3, 4)
        combine(5, 5, 0, True, False)
        mask(3, 3)
        warm(2)
        flip_w(3, 3)
        combine(3, 5, 0, False, False)
        quantise_w(3, 4)
        multiply(3, 4, 0)
        flip_chain(0, (0,))
        quantise_w(3, 3)
        mask(4, 4)
        combine(3, 4, 0, True, False)
        flip_w(4, 4)
        multiply(3, 3, 0)
        quantise_chain(0, 0)
        mask(4, 5)
        combine(3, 3, 0, True, True)
        quantise_w(4, 4)
        flip_w(4, 5)
        spread_bias(1)
        flip_z(1, (2, 1, 0))
        quantise_w(4, 5)
        quantise_chain(1, 0)
        multiply(4, 4, 0)
        multiply(4, 5, 0)
        quantise_z(1, (2, 1, 0))
        combine(4, 4, 0, False, True)
        keep_bias(1)
        flip_chain(1, (2, 1))
        combine(4, 5, 0, False, True)
        flip_c(0)
        multiply(5, 5, 1)
        multiply(3, 5, 1)
        multiply(3, 4, 1)
        multiply(3, 3, 1)
        quantise_chain(2, 0)
        combine(5, 5, 1, True, False)
        quantise_c(0)
        combine(3, 5, 1, False, False)
        combine(3, 4, 1, True, False)
        combine(3, 3, 1, True, True)
        flip_chain(1, (0,))
        flip_c(1)
        multiply(4, 4, 1)
        multiply(4, 5, 1)
        project(0, 0)
        combine(4, 4, 1, False, True)
        quantise_c(1)
        combine(4, 5, 1, False, True)
        flip_c(2)
        quantise_chain(1, 1)
        quantise_chain(0, 1)
        project(1, 0)
        quantise_chain(2, 1)
        finish(0, 0)
        quantise_c(2)
        finish(1, 0)
        project(0, 1)
        project(1, 1)
        finish(0, 1)
        finish(1, 1)
        halves = OUTS // PAIR
        flip_c(3)
        flip_c(4)
        project(2, 0)
        project(2, 1)
        quantise_c(3)
        finish(2, 0)
        finish(2, 1)
        quantise_c(4)
        flip_c(5)
        flip_c(6)
        for r in (3, 4):
            for pair in range(2):
                project(r, pair)
        quantise_c(5)
        finish(3, 0)
        finish(3, 1)
        quantise_c(6)
        finish(4, 0)
        finish(4, 1)
        flip_c(7)
        for r in (5, 6):
            for pair in range(2):
                project(r, pair)
        quantise_c(7)
        finish(5, 0)
        finish(5, 1)
        finish(6, 0)
        finish(6, 1)
        for pair in range(2):
            project(7, pair)
            finish(7, pair)
